import numpy as np
import ml_dtypes


def mxq(x, axis, fmt="e4m3"):
    dtype, down = {"e4m3": (ml_dtypes.float8_e4m3fn, 7), "e5m2": (ml_dtypes.float8_e5m2, 14)}[fmt]
    v = np.moveaxis(np.asarray(x, np.float32).astype(ml_dtypes.bfloat16).astype(np.float64), axis, -1)
    blocks = v.reshape(v.shape[:-1] + (-1, 32))
    amax = np.abs(blocks).max(-1, keepdims=True)
    byte = np.maximum(np.where(amax > 0, np.frexp(amax)[1] - 1 + 127, 0) - down, 1)
    scale = np.exp2(byte - 127.0)
    codes = (blocks / scale).astype(np.float32).astype(dtype).astype(np.float64)
    return np.moveaxis((codes * scale).reshape(v.shape), -1, axis)


WIDE = False


def mx_kscale(k):
    if not WIDE:
        return np.ones(k)
    levels = np.array([10, -10, 5, -5, 0])
    a = np.random.permutation(np.resize(levels, k // 512 * 4)).reshape(k // 512, 4)
    idx = np.arange(k)
    return np.exp2(a[idx // 512, idx % 128 // 32])


BF16 = ml_dtypes.bfloat16


def bf(x):
    return np.asarray(x, np.float32).astype(BF16)


def f64(x):
    return np.asarray(x).astype(np.float64)


E2M1 = np.array([0.0, 0.5, 1.0, 1.5, 2.0, 3.0, 4.0, 6.0, -0.0, -0.5, -1.0, -1.5, -2.0, -3.0, -4.0, -6.0])


def pack_weight(w, fmt):
    k, n = w.shape
    w = f64(bf(w)).reshape(k // 32, 32, n)
    amax = np.abs(w).max(1)
    if fmt == "e4m3":
        byte = np.frexp(amax)[1] - 1 + 127 - 7
    else:
        mant, ex = np.frexp(amax / 6.0)
        byte = np.where(mant > 0.5, ex, ex - 1) + 127
    byte = np.clip(np.where(amax > 0, byte, 1), 1, 254)
    scaled = (w * np.exp2(127.0 - byte)[:, None, :]).reshape(k, n).astype(np.float32)
    by_word = np.ascontiguousarray(scaled.reshape(k // 512, 128, 4, n).transpose(0, 1, 3, 2))
    if fmt == "e4m3":
        words = by_word.astype(ml_dtypes.float8_e4m3fn).view(np.uint8)
    else:
        c = by_word.astype(ml_dtypes.float4_e2m1fn).view(np.uint8) & 0xF
        words = c[..., 0::2] | (c[..., 1::2] << 4)
    return np.ascontiguousarray(words), np.ascontiguousarray(byte.astype(np.uint8).reshape(k // 512, 16, n))


def unpack_weight(words, scales, fmt):
    g, p, n, _ = words.shape
    if fmt == "e4m3":
        vals = np.ascontiguousarray(words).view(ml_dtypes.float8_e4m3fn).astype(np.float64)
    else:
        nib = np.empty((g, p, n, 4), np.uint8)
        nib[..., 0::2] = words & 0xF
        nib[..., 1::2] = words >> 4
        vals = E2M1[nib]
    vals = vals * np.repeat(np.exp2(scales.astype(np.float64) - 127.0), 8, axis=1)[..., None]
    return vals.transpose(0, 1, 3, 2).reshape(g * 512, n)

def pack4(w):
    words, scales = pack_weight(w, "e2m1")
    return words.reshape(words.shape[0], 128, -1), scales


def unpack4(words, scales):
    return unpack_weight(words.reshape(words.shape[0], 128, -1, 2), scales, "e2m1")


B, IN, L = 128, 1024, 640


def sigmoid(v):
    return 1.0 / (1.0 + np.exp(-v))


def setup_inputs():
    s = mx_kscale(IN)
    inp = bf(np.random.standard_normal((B, IN)) * s)
    h0 = bf(np.random.standard_normal((B, L)))
    gh0 = bf(np.random.standard_normal((B, 3 * L)) * 0.75)
    w = np.random.standard_normal((3 * L, IN)) * 0.7 / np.sqrt(IN) / s
    words, scales = pack4(w.T)
    b_ih0 = bf(np.random.standard_normal(3 * L) * 0.3)
    return {"input": inp,
            "h0": h0,
            "gh0": gh0,
            "W_ih0_words": words,
            "W_ih0_scales": scales,
            "b_ih0": b_ih0}


def reference(input, h0, gh0, W_ih0_words, W_ih0_scales, b_ih0):
    h, gh = f64(h0), f64(gh0)
    gi = (mxq(f64(input), 1, "e4m3") @ unpack4(W_ih0_words, W_ih0_scales)) + f64(b_ih0)
    i_r, i_z, i_n = gi[:, :L], gi[:, L:2 * L], gi[:, 2 * L:]
    h_r, h_z, h_n = gh[:, :L], gh[:, L:2 * L], gh[:, 2 * L:]
    r = sigmoid(i_r + h_r)
    z = sigmoid(i_z + h_z)
    n = np.tanh(i_n + r * h_n)
    return (1.0 - z) * n + z * h

@@ -1,0 +1,141 @@
+from contextlib import ExitStack
+
+import concourse.mybir as mybir
+from concourse.masks import make_identity
+
+F32 = mybir.dt.float32
+BF16 = mybir.dt.bfloat16
+I32 = mybir.dt.int32
+U32 = mybir.dt.uint32
+U8 = mybir.dt.uint8
+FP8X4 = mybir.dt.float8_e4m3fn_x4
+FP4X4 = mybir.dt.float4_e2m1fn_x4
+ACT = mybir.ActivationFunctionType
+ALU = mybir.AluOpType
+
+P = 128
+PACK = 4
+K = 1024
+PASSES = K // (P * PACK)
+L = 640
+GATE_R, GATE_Z, GATE_N = 0, 1, 2
+GATES = 3
+
+CHUNKS = ((0, 512), (512, 128))
+
+FLOPS = 2 * P * K * GATES * L
+
+
+def tile_grucellstack_pa_s_kernel(tc, x, h0, gh0, w_words, w_scales, b_ih0, out):
+    nc = tc.nc
+    with ExitStack() as ctx:
+        keep = ctx.enter_context(tc.tile_pool(name="keep", bufs=1))
+        psum = ctx.enter_context(tc.psum_pool(name="psum", bufs=1))
+
+        w_planes = keep.tile([P, PASSES, GATES * L], U8, align_bytes=64)
+        nc.vector.memset(w_planes[:].rearrange("p g n -> p (g n)").bitcast(I32), 0)
+        identity = keep.tile([P, P], F32)
+        make_identity(nc, identity[:])
+        warm = keep.tile([P, 1], F32)
+        nc.gpsimd.memset(warm[:], 0.0)
+        nc.scalar.activation(out=warm[:], in_=warm[:], func=ACT.Sigmoid)
+
+        x_sb = keep.tile([P, K], BF16)
+        nc.sync.dma_start(out=x_sb[:], in_=x)
+        scale_rows = w_scales.rearrange("g q n -> q g n")
+        for r in range(4):
+            nc.sync.dma_start(
+                out=w_planes[r:P:32, :, :].bitcast(I32),
+                in_=scale_rows[r:16:4, :, :].bitcast(I32),
+            )
+        w_sb = keep.tile([P, PASSES, 2 * GATES * L], U8, align_bytes=64)
+        word_rows = w_words.rearrange("g p n -> p g n")
+        for gate in (GATE_R, GATE_N, GATE_Z):
+            gate_bytes = slice(2 * L * gate, 2 * L * (gate + 1))
+            nc.sync.dma_start(
+                out=w_sb[:, :, gate_bytes].bitcast(I32),
+                in_=word_rows[:, :, gate_bytes].bitcast(I32),
+            )
+        gh_sb = keep.tile([P, GATES * L], BF16)
+        nc.scalar.dma_start(out=gh_sb[:], in_=gh0)
+        bias_sb = keep.tile([P, GATES * L], BF16)
+        nc.scalar.dma_start(out=bias_sb[:], in_=b_ih0.partition_broadcast(P))
+        h_sb = keep.tile([P, L], BF16)
+        nc.scalar.dma_start(out=h_sb[:], in_=h0)
+
+        x_words = x_sb[:].bitcast(F32)
+        grouped = keep.tile([P, PASSES, P, PACK], BF16, align_bytes=64)
+        for g in range(PASSES):
+            x_t = psum.tile([P, 2, P], F32, name="x_t%d" % g)
+            for u in range(2):
+                nc.tensor.transpose(
+                    x_t[:, u, :], x_words[:, 256 * g + u : 256 * (g + 1) : 2], identity[:]
+                )
+            pairs = grouped[:, g].rearrange("p b t -> p (b t)").bitcast(F32)
+            copy = nc.vector.tensor_copy if g == 0 else nc.scalar.copy
+            copy(
+                out=pairs.rearrange("p (b u) -> p b u", u=2),
+                in_=x_t[:].rearrange("p u b -> p b u"),
+            )
+        x_codes = keep.tile([P, PASSES, P], U32, align_bytes=64)
+        x_planes = keep.tile([P, PASSES, P], U8, align_bytes=64)
+        nc.vector.quantize_mx(
+            out=x_codes[:].rearrange("p g b -> p (g b)").bitcast(FP8X4),
+            scales=x_planes[:].rearrange("p g b -> p (g b)"),
+            in_=grouped[:].rearrange("p g b t -> p (g b t)"),
+        )
+
+        ghb = keep.tile([P, 2 * L], F32)
+        nc.vector.tensor_add(out=ghb[:, 0:L], in0=gh_sb[:, 0:L], in1=bias_sb[:, 0:L])
+        nc.gpsimd.tensor_add(
+            out=ghb[:, L : 2 * L], in0=gh_sb[:, L : 2 * L], in1=bias_sb[:, L : 2 * L]
+        )
+
+        gi = {}
+        for gate in (GATE_R, GATE_N, GATE_Z):
+            for start, width in CHUNKS:
+                acc = psum.tile([P, width], F32, name="gi%d_%d" % (gate, start))
+                gi[(gate, start)] = acc
+                first = gate * L + start
+                for g in range(PASSES):
+                    nc.tensor.matmul_mx(
+                        out=acc[:],
+                        lhsT=x_codes[:, g, :].bitcast(FP8X4),
+                        lhsT_scale=x_planes[:, g, :],
+                        rhs=w_sb[:, g, 2 * first : 2 * (first + width)].bitcast(FP4X4),
+                        rhs_scale=w_planes[:, g, first : first + width],
+                        start=(g == 0),
+                        stop=(g == PASSES - 1),
+                    )
+
+        pre_r = keep.tile([P, L], F32)
+        pre_z = keep.tile([P, L], F32)
+        pre_n = keep.tile([P, L], F32)
+        gate_r = keep.tile([P, L], F32)
+        gate_z = keep.tile([P, L], F32)
+        one_minus_z = keep.tile([P, L], F32)
+        gate_n = keep.tile([P, L], F32)
+        r_gh = keep.tile([P, L], F32)
+        z_h = keep.tile([P, L], F32)
+        blend = keep.tile([P, L], F32)
+        for start, width in CHUNKS:
+            cols = slice(start, start + width)
+            z_cols = slice(L + start, L + start + width)
+            n_cols = slice(2 * L + start, 2 * L + start + width)
+            nc.vector.tensor_add(out=pre_r[:, cols], in0=gi[(GATE_R, start)][:], in1=ghb[:, cols])
+            nc.scalar.activation(out=gate_r[:, cols], in_=pre_r[:, cols], func=ACT.Sigmoid)
+            nc.vector.tensor_add(
+                out=pre_n[:, cols], in0=gi[(GATE_N, start)][:], in1=bias_sb[:, n_cols]
+            )
+            nc.vector.tensor_add(out=pre_z[:, cols], in0=gi[(GATE_Z, start)][:], in1=ghb[:, z_cols])
+            nc.scalar.activation(out=gate_z[:, cols], in_=pre_z[:, cols], func=ACT.Sigmoid)
+            nc.scalar.activation(
+                out=one_minus_z[:, cols], in_=pre_z[:, cols], func=ACT.Sigmoid, scale=-1.0
+            )
+            nc.vector.tensor_mul(out=r_gh[:, cols], in0=gate_r[:, cols], in1=gh_sb[:, n_cols])
+            nc.vector.tensor_add(out=pre_n[:, cols], in0=pre_n[:, cols], in1=r_gh[:, cols])
+            nc.scalar.activation(out=gate_n[:, cols], in_=pre_n[:, cols], func=ACT.Tanh)
+            nc.gpsimd.tensor_mul(out=z_h[:, cols], in0=gate_z[:, cols], in1=h_sb[:, cols])
+            nc.vector.tensor_mul(out=blend[:, cols], in0=one_minus_z[:, cols], in1=gate_n[:, cols])
+            nc.vector.tensor_add(out=blend[:, cols], in0=blend[:, cols], in1=z_h[:, cols])
+            nc.sync.dma_start(out=out[:, cols], in_=blend[:, cols])

@@ -11,7 +11,6 @@ U8 = mybir.dt.uint8
 FP8X4 = mybir.dt.float8_e4m3fn_x4
 FP4X4 = mybir.dt.float4_e2m1fn_x4
 ACT = mybir.ActivationFunctionType
-ALU = mybir.AluOpType
 
 P = 128
 PACK = 4
@@ -20,6 +19,10 @@ PASSES = K // (P * PACK)
 L = 640
 GATE_R, GATE_Z, GATE_N = 0, 1, 2
 GATES = 3
+BANK_F32 = 512
+BANK_BF16 = 2 * BANK_F32
+PER_BANK = BANK_F32 // P
+BIAS_BANKS = 2
 
 CHUNKS = ((0, 512), (512, 128))
 
@@ -29,15 +32,29 @@ FLOPS = 2 * P * K * GATES * L
 def tile_grucellstack_pa_s_kernel(tc, x, h0, gh0, w_words, w_scales, b_ih0, out):
     nc = tc.nc
     with ExitStack() as ctx:
+        ctx.enter_context(tc.manual_schedule())
         keep = ctx.enter_context(tc.tile_pool(name="keep", bufs=1))
-        psum = ctx.enter_context(tc.psum_pool(name="psum", bufs=1))
+        bias_psum = ctx.enter_context(tc.psum_pool(name="bias_psum", bufs=1))
 
+        bias_rows = keep.tile([P, P], F32)
+        nc.vector.memset(bias_rows[:], 0.0)
         w_planes = keep.tile([P, PASSES, GATES * L], U8, align_bytes=64)
         nc.vector.memset(w_planes[:].rearrange("p g n -> p (g n)").bitcast(I32), 0)
-        identity = keep.tile([P, P], F32)
-        make_identity(nc, identity[:])
         warm = keep.tile([P, 1], F32)
         nc.gpsimd.memset(warm[:], 0.0)
+        identity = keep.tile([P, P], F32)
+        make_identity(nc, identity[:])
+
+        full_rows = (GATES * L) // (2 * P)
+        bias_pairs = bias_rows[:].bitcast(BF16)
+        nc.scalar.dma_start(
+            out=bias_pairs[0:full_rows, :],
+            in_=b_ih0[0 : full_rows * 2 * P].rearrange("(c j) -> c j", j=2 * P),
+        )
+        nc.scalar.dma_start(
+            out=bias_pairs[full_rows : full_rows + 1, 0:P],
+            in_=b_ih0[full_rows * 2 * P : GATES * L].rearrange("(c j) -> c j", j=P),
+        )
         nc.scalar.activation(out=warm[:], in_=warm[:], func=ACT.Sigmoid)
 
         x_sb = keep.tile([P, K], BF16)
@@ -50,56 +67,77 @@ def tile_grucellstack_pa_s_kernel(tc, x, h0, gh0, w_words, w_scales, b_ih0, out)
             )
         w_sb = keep.tile([P, PASSES, 2 * GATES * L], U8, align_bytes=64)
         word_rows = w_words.rearrange("g p n -> p g n")
-        for gate in (GATE_R, GATE_N, GATE_Z):
+        gh_sb = keep.tile([P, GATES * L], BF16)
+        h_sb = keep.tile([P, L], BF16)
+
+        def load_words(gate):
             gate_bytes = slice(2 * L * gate, 2 * L * (gate + 1))
             nc.sync.dma_start(
                 out=w_sb[:, :, gate_bytes].bitcast(I32),
                 in_=word_rows[:, :, gate_bytes].bitcast(I32),
             )
-        gh_sb = keep.tile([P, GATES * L], BF16)
-        nc.scalar.dma_start(out=gh_sb[:], in_=gh0)
-        bias_sb = keep.tile([P, GATES * L], BF16)
-        nc.scalar.dma_start(out=bias_sb[:], in_=b_ih0.partition_broadcast(P))
-        h_sb = keep.tile([P, L], BF16)
-        nc.scalar.dma_start(out=h_sb[:], in_=h0)
 
-        x_words = x_sb[:].bitcast(F32)
+        load_words(GATE_R)
+        nc.sync.dma_start(out=gh_sb[:], in_=gh0)
+        load_words(GATE_Z)
+        load_words(GATE_N)
+        nc.sync.dma_start(out=h_sb[:], in_=h0)
+
+        bias_cols = keep.tile([P, BIAS_BANKS * PER_BANK], F32)
         grouped = keep.tile([P, PASSES, P, PACK], BF16, align_bytes=64)
-        for g in range(PASSES):
-            x_t = psum.tile([P, 2, P], F32, name="x_t%d" % g)
-            for u in range(2):
-                nc.tensor.transpose(
-                    x_t[:, u, :], x_words[:, 256 * g + u : 256 * (g + 1) : 2], identity[:]
-                )
-            pairs = grouped[:, g].rearrange("p b t -> p (b t)").bitcast(F32)
-            copy = nc.vector.tensor_copy if g == 0 else nc.scalar.copy
-            copy(
-                out=pairs.rearrange("p (b u) -> p b u", u=2),
-                in_=x_t[:].rearrange("p u b -> p b u"),
-            )
         x_codes = keep.tile([P, PASSES, P], U32, align_bytes=64)
         x_planes = keep.tile([P, PASSES, P], U8, align_bytes=64)
-        nc.vector.quantize_mx(
-            out=x_codes[:].rearrange("p g b -> p (g b)").bitcast(FP8X4),
-            scales=x_planes[:].rearrange("p g b -> p (g b)"),
-            in_=grouped[:].rearrange("p g b t -> p (g b t)"),
-        )
+        with tc.psum_pool(name="head_psum", bufs=1) as head_psum:
+            bias_t = head_psum.tile([P, P], F32)
+            nc.tensor.transpose(bias_t[:], bias_rows[:], identity[:])
+            nc.scalar.copy(out=bias_cols[:], in_=bias_t[:, 0 : BIAS_BANKS * PER_BANK])
+            x_words = x_sb[:].bitcast(F32)
+            for g in range(PASSES):
+                x_t = head_psum.tile([P, 2, P], F32, name="x_t%d" % g)
+                for u in range(2):
+                    nc.tensor.transpose(
+                        x_t[:, u, :], x_words[:, 256 * g + u : 256 * (g + 1) : 2], identity[:]
+                    )
+                pairs = grouped[:, g].rearrange("p b t -> p (b t)").bitcast(F32)
+                nc.scalar.copy(
+                    out=pairs.rearrange("p (b u) -> p b u", u=2),
+                    in_=x_t[:].rearrange("p u b -> p b u"),
+                )
+                nc.vector.quantize_mx(
+                    out=x_codes[:, g, :].bitcast(FP8X4),
+                    scales=x_planes[:, g, :],
+                    in_=grouped[:, g].rearrange("p b t -> p (b t)"),
+                )
 
-        ghb = keep.tile([P, 2 * L], F32)
-        nc.vector.tensor_add(out=ghb[:, 0:L], in0=gh_sb[:, 0:L], in1=bias_sb[:, 0:L])
-        nc.gpsimd.tensor_add(
-            out=ghb[:, L : 2 * L], in0=gh_sb[:, L : 2 * L], in1=bias_sb[:, L : 2 * L]
-        )
+        bias_banks = [
+            bias_psum.tile([P, BANK_F32], F32, name="bias_bank%d" % i) for i in range(BIAS_BANKS)
+        ]
 
+        def spread_bias(bank):
+            for i in range(PER_BANK):
+                c = PER_BANK * bank + i
+                nc.tensor.transpose(
+                    bias_banks[bank][:, P * i : P * (i + 1)],
+                    bias_cols[:, c : c + 1].to_broadcast([P, P]),
+                    identity[:],
+                )
+
+        def bias(first, width):
+            bank = first // BANK_BF16
+            assert first + width <= (bank + 1) * BANK_BF16
+            return bias_banks[bank][:].bitcast(BF16)[:, first % BANK_BF16 : first % BANK_BF16 + width]
+
+        gi_psum = ctx.enter_context(tc.psum_pool(name="gi_psum", bufs=1, reuse_waits="tile"))
         gi = {}
-        for gate in (GATE_R, GATE_N, GATE_Z):
+
+        def multiply(gate):
             for start, width in CHUNKS:
-                acc = psum.tile([P, width], F32, name="gi%d_%d" % (gate, start))
-                gi[(gate, start)] = acc
-                first = gate * L + start
-                for g in range(PASSES):
+                gi[(gate, start)] = gi_psum.tile([P, width], F32, name="gi%d_%d" % (gate, start))
+            for g in range(PASSES):
+                for start, width in CHUNKS:
+                    first = gate * L + start
                     nc.tensor.matmul_mx(
-                        out=acc[:],
+                        out=gi[(gate, start)][:],
                         lhsT=x_codes[:, g, :].bitcast(FP8X4),
                         lhsT_scale=x_planes[:, g, :],
                         rhs=w_sb[:, g, 2 * first : 2 * (first + width)].bitcast(FP4X4),
@@ -108,6 +146,13 @@ def tile_grucellstack_pa_s_kernel(tc, x, h0, gh0, w_words, w_scales, b_ih0, out)
                         stop=(g == PASSES - 1),
                     )
 
+        spread_bias(0)
+        multiply(GATE_R)
+        spread_bias(1)
+        multiply(GATE_Z)
+        multiply(GATE_N)
+
+        ghb = keep.tile([P, 2 * L], F32)
         pre_r = keep.tile([P, L], F32)
         pre_z = keep.tile([P, L], F32)
         pre_n = keep.tile([P, L], F32)
@@ -115,27 +160,43 @@ def tile_grucellstack_pa_s_kernel(tc, x, h0, gh0, w_words, w_scales, b_ih0, out)
         gate_z = keep.tile([P, L], F32)
         one_minus_z = keep.tile([P, L], F32)
         gate_n = keep.tile([P, L], F32)
-        r_gh = keep.tile([P, L], F32)
         z_h = keep.tile([P, L], F32)
         blend = keep.tile([P, L], F32)
+
+        def add_bias_to_gh(first, width):
+            cols = slice(first, first + width)
+            nc.vector.tensor_add(out=ghb[:, cols], in0=bias(first, width), in1=gh_sb[:, cols])
+
+        add_bias_to_gh(0, L)
+        for start, width in CHUNKS:
+            cols = slice(start, start + width)
+            nc.vector.tensor_add(out=pre_r[:, cols], in0=gi[(GATE_R, start)][:], in1=ghb[:, cols])
+            nc.scalar.activation(out=gate_r[:, cols], in_=pre_r[:, cols], func=ACT.Sigmoid)
+
+        add_bias_to_gh(L, BANK_BF16 - L)
+        add_bias_to_gh(BANK_BF16, 2 * L - BANK_BF16)
         for start, width in CHUNKS:
             cols = slice(start, start + width)
             z_cols = slice(L + start, L + start + width)
-            n_cols = slice(2 * L + start, 2 * L + start + width)
-            nc.vector.tensor_add(out=pre_r[:, cols], in0=gi[(GATE_R, start)][:], in1=ghb[:, cols])
-            nc.scalar.activation(out=gate_r[:, cols], in_=pre_r[:, cols], func=ACT.Sigmoid)
-            nc.vector.tensor_add(
-                out=pre_n[:, cols], in0=gi[(GATE_N, start)][:], in1=bias_sb[:, n_cols]
-            )
             nc.vector.tensor_add(out=pre_z[:, cols], in0=gi[(GATE_Z, start)][:], in1=ghb[:, z_cols])
             nc.scalar.activation(out=gate_z[:, cols], in_=pre_z[:, cols], func=ACT.Sigmoid)
             nc.scalar.activation(
                 out=one_minus_z[:, cols], in_=pre_z[:, cols], func=ACT.Sigmoid, scale=-1.0
             )
-            nc.vector.tensor_mul(out=r_gh[:, cols], in0=gate_r[:, cols], in1=gh_sb[:, n_cols])
-            nc.vector.tensor_add(out=pre_n[:, cols], in0=pre_n[:, cols], in1=r_gh[:, cols])
-            nc.scalar.activation(out=gate_n[:, cols], in_=pre_n[:, cols], func=ACT.Tanh)
             nc.gpsimd.tensor_mul(out=z_h[:, cols], in0=gate_z[:, cols], in1=h_sb[:, cols])
+
+        for start, width in CHUNKS:
+            cols = slice(start, start + width)
+            n_cols = slice(2 * L + start, 2 * L + start + width)
+            nc.vector.tensor_mul(out=pre_n[:, cols], in0=gate_r[:, cols], in1=gh_sb[:, n_cols])
+            nc.vector.tensor_add(
+                out=pre_n[:, cols], in0=bias(2 * L + start, width), in1=pre_n[:, cols]
+            )
+            nc.vector.tensor_add(out=pre_n[:, cols], in0=gi[(GATE_N, start)][:], in1=pre_n[:, cols])
+            nc.scalar.activation(out=gate_n[:, cols], in_=pre_n[:, cols], func=ACT.Tanh)
+
+        for start, width in CHUNKS:
+            cols = slice(start, start + width)
             nc.vector.tensor_mul(out=blend[:, cols], in0=one_minus_z[:, cols], in1=gate_n[:, cols])
             nc.vector.tensor_add(out=blend[:, cols], in0=blend[:, cols], in1=z_h[:, cols])
             nc.sync.dma_start(out=out[:, cols], in_=blend[:, cols])

@@ -23,6 +23,10 @@ BANK_F32 = 512
 BANK_BF16 = 2 * BANK_F32
 PER_BANK = BANK_F32 // P
 BIAS_BANKS = 2
+BIAS_ROWS = BIAS_BANKS * PER_BANK
+ROW_WORDS = GATES * L // (2 * BIAS_ROWS)
+BANK_BIAS = 2 * ROW_WORDS * PER_BANK
+IDLE_MATMULS = 4
 
 CHUNKS = ((0, 512), (512, 128))
 
@@ -40,47 +44,49 @@ def tile_grucellstack_pa_s_kernel(tc, x, h0, gh0, w_words, w_scales, b_ih0, out)
         nc.vector.memset(bias_rows[:], 0.0)
         w_planes = keep.tile([P, PASSES, GATES * L], U8, align_bytes=64)
         nc.vector.memset(w_planes[:].rearrange("p g n -> p (g n)").bitcast(I32), 0)
+        idle_work = keep.tile([P, P], F32)
+        nc.gpsimd.memset(idle_work[:], 0.0)
         warm = keep.tile([P, 1], F32)
         nc.gpsimd.memset(warm[:], 0.0)
         identity = keep.tile([P, P], F32)
         make_identity(nc, identity[:])
-
-        full_rows = (GATES * L) // (2 * P)
-        bias_pairs = bias_rows[:].bitcast(BF16)
-        nc.scalar.dma_start(
-            out=bias_pairs[0:full_rows, :],
-            in_=b_ih0[0 : full_rows * 2 * P].rearrange("(c j) -> c j", j=2 * P),
-        )
-        nc.scalar.dma_start(
-            out=bias_pairs[full_rows : full_rows + 1, 0:P],
-            in_=b_ih0[full_rows * 2 * P : GATES * L].rearrange("(c j) -> c j", j=P),
-        )
         nc.scalar.activation(out=warm[:], in_=warm[:], func=ACT.Sigmoid)
 
         x_sb = keep.tile([P, K], BF16)
         nc.sync.dma_start(out=x_sb[:], in_=x)
+        nc.sync.dma_start(
+            out=bias_rows[:].bitcast(BF16)[0:BIAS_ROWS, 0 : 2 * ROW_WORDS],
+            in_=b_ih0.rearrange("(c j) -> c j", j=2 * ROW_WORDS),
+        )
+
+        word_rows = w_words.rearrange("g p n -> p g n")
+        w_sb = {}
+        gh_sb = {}
+
+        def load_words(gate):
+            w_sb[gate] = keep.tile([P, PASSES, 2 * L], U8, align_bytes=64, name="w_sb%d" % gate)
+            nc.sync.dma_start(
+                out=w_sb[gate][:].bitcast(I32),
+                in_=word_rows[:, :, 2 * L * gate : 2 * L * (gate + 1)].bitcast(I32),
+            )
+
+        def load_gh(gate):
+            gh_sb[gate] = keep.tile([P, L], BF16, name="gh_sb%d" % gate)
+            nc.sync.dma_start(out=gh_sb[gate][:], in_=gh0[:, L * gate : L * (gate + 1)])
+
+        load_gh(GATE_R)
+        load_words(GATE_R)
         scale_rows = w_scales.rearrange("g q n -> q g n")
         for r in range(4):
             nc.sync.dma_start(
                 out=w_planes[r:P:32, :, :].bitcast(I32),
                 in_=scale_rows[r:16:4, :, :].bitcast(I32),
             )
-        w_sb = keep.tile([P, PASSES, 2 * GATES * L], U8, align_bytes=64)
-        word_rows = w_words.rearrange("g p n -> p g n")
-        gh_sb = keep.tile([P, GATES * L], BF16)
-        h_sb = keep.tile([P, L], BF16)
-
-        def load_words(gate):
-            gate_bytes = slice(2 * L * gate, 2 * L * (gate + 1))
-            nc.sync.dma_start(
-                out=w_sb[:, :, gate_bytes].bitcast(I32),
-                in_=word_rows[:, :, gate_bytes].bitcast(I32),
-            )
-
-        load_words(GATE_R)
-        nc.sync.dma_start(out=gh_sb[:], in_=gh0)
         load_words(GATE_Z)
+        load_gh(GATE_Z)
         load_words(GATE_N)
+        load_gh(GATE_N)
+        h_sb = keep.tile([P, L], BF16)
         nc.sync.dma_start(out=h_sb[:], in_=h0)
 
         bias_cols = keep.tile([P, BIAS_BANKS * PER_BANK], F32)
@@ -88,21 +94,29 @@ def tile_grucellstack_pa_s_kernel(tc, x, h0, gh0, w_words, w_scales, b_ih0, out)
         x_codes = keep.tile([P, PASSES, P], U32, align_bytes=64)
         x_planes = keep.tile([P, PASSES, P], U8, align_bytes=64)
         with tc.psum_pool(name="head_psum", bufs=1) as head_psum:
-            bias_t = head_psum.tile([P, P], F32)
-            nc.tensor.transpose(bias_t[:], bias_rows[:], identity[:])
-            nc.scalar.copy(out=bias_cols[:], in_=bias_t[:, 0 : BIAS_BANKS * PER_BANK])
+            idle_out = head_psum.tile([P, P], F32)
+            for i in range(IDLE_MATMULS):
+                nc.tensor.matmul(
+                    out=idle_out[:], lhsT=idle_work[:], rhs=idle_work[:], start=True, stop=True
+                )
             x_words = x_sb[:].bitcast(F32)
+            x_t = {}
             for g in range(PASSES):
-                x_t = head_psum.tile([P, 2, P], F32, name="x_t%d" % g)
+                x_t[g] = head_psum.tile([P, 2, P], F32, name="x_t%d" % g)
                 for u in range(2):
                     nc.tensor.transpose(
-                        x_t[:, u, :], x_words[:, 256 * g + u : 256 * (g + 1) : 2], identity[:]
+                        x_t[g][:, u, :], x_words[:, 256 * g + u : 256 * (g + 1) : 2], identity[:]
                     )
+            bias_t = head_psum.tile([P, P], F32)
+            nc.tensor.transpose(bias_t[:], bias_rows[:], identity[:])
+            nc.vector.tensor_copy(out=bias_cols[:], in_=bias_t[:, 0 : BIAS_BANKS * PER_BANK])
+            for g in range(PASSES):
                 pairs = grouped[:, g].rearrange("p b t -> p (b t)").bitcast(F32)
                 nc.scalar.copy(
                     out=pairs.rearrange("p (b u) -> p b u", u=2),
-                    in_=x_t[:].rearrange("p u b -> p b u"),
+                    in_=x_t[g][:].rearrange("p u b -> p b u"),
                 )
+            for g in range(PASSES):
                 nc.vector.quantize_mx(
                     out=x_codes[:, g, :].bitcast(FP8X4),
                     scales=x_planes[:, g, :],
@@ -117,15 +131,16 @@ def tile_grucellstack_pa_s_kernel(tc, x, h0, gh0, w_words, w_scales, b_ih0, out)
             for i in range(PER_BANK):
                 c = PER_BANK * bank + i
                 nc.tensor.transpose(
-                    bias_banks[bank][:, P * i : P * (i + 1)],
+                    bias_banks[bank][:, ROW_WORDS * i : ROW_WORDS * i + P],
                     bias_cols[:, c : c + 1].to_broadcast([P, P]),
                     identity[:],
                 )
 
         def bias(first, width):
-            bank = first // BANK_BF16
-            assert first + width <= (bank + 1) * BANK_BF16
-            return bias_banks[bank][:].bitcast(BF16)[:, first % BANK_BF16 : first % BANK_BF16 + width]
+            bank = first // BANK_BIAS
+            at = first - bank * BANK_BIAS
+            assert at + width <= BANK_BIAS
+            return bias_banks[bank][:].bitcast(BF16)[:, at : at + width]
 
         gi_psum = ctx.enter_context(tc.psum_pool(name="gi_psum", bufs=1, reuse_waits="tile"))
         gi = {}
@@ -140,21 +155,23 @@ def tile_grucellstack_pa_s_kernel(tc, x, h0, gh0, w_words, w_scales, b_ih0, out)
                         out=gi[(gate, start)][:],
                         lhsT=x_codes[:, g, :].bitcast(FP8X4),
                         lhsT_scale=x_planes[:, g, :],
-                        rhs=w_sb[:, g, 2 * first : 2 * (first + width)].bitcast(FP4X4),
+                        rhs=w_sb[gate][:, g, 2 * start : 2 * (start + width)].bitcast(FP4X4),
                         rhs_scale=w_planes[:, g, first : first + width],
                         start=(g == 0),
                         stop=(g == PASSES - 1),
                     )
 
         spread_bias(0)
-        multiply(GATE_R)
         spread_bias(1)
+        multiply(GATE_R)
         multiply(GATE_Z)
         multiply(GATE_N)
 
         ghb = keep.tile([P, 2 * L], F32)
+        bias_n = keep.tile([P, L], BF16)
         pre_r = keep.tile([P, L], F32)
         pre_z = keep.tile([P, L], F32)
+        gi_b_n = keep.tile([P, L], F32)
         pre_n = keep.tile([P, L], F32)
         gate_r = keep.tile([P, L], F32)
         gate_z = keep.tile([P, L], F32)
@@ -163,36 +180,42 @@ def tile_grucellstack_pa_s_kernel(tc, x, h0, gh0, w_words, w_scales, b_ih0, out)
         z_h = keep.tile([P, L], F32)
         blend = keep.tile([P, L], F32)
 
-        def add_bias_to_gh(first, width):
-            cols = slice(first, first + width)
-            nc.vector.tensor_add(out=ghb[:, cols], in0=bias(first, width), in1=gh_sb[:, cols])
+        def add_bias_to_gh(gate, start, width):
+            first = gate * L + start
+            nc.vector.tensor_add(
+                out=ghb[:, first : first + width],
+                in0=bias(first, width),
+                in1=gh_sb[gate][:, start : start + width],
+            )
 
-        add_bias_to_gh(0, L)
+        add_bias_to_gh(GATE_R, 0, L)
+        nc.scalar.copy(out=bias_n[:], in_=bias(GATE_N * L, L))
         for start, width in CHUNKS:
             cols = slice(start, start + width)
             nc.vector.tensor_add(out=pre_r[:, cols], in0=gi[(GATE_R, start)][:], in1=ghb[:, cols])
             nc.scalar.activation(out=gate_r[:, cols], in_=pre_r[:, cols], func=ACT.Sigmoid)
 
-        add_bias_to_gh(L, BANK_BF16 - L)
-        add_bias_to_gh(BANK_BF16, 2 * L - BANK_BF16)
+        add_bias_to_gh(GATE_Z, 0, BANK_BIAS - L)
+        add_bias_to_gh(GATE_Z, BANK_BIAS - L, 2 * L - BANK_BIAS)
         for start, width in CHUNKS:
             cols = slice(start, start + width)
             z_cols = slice(L + start, L + start + width)
             nc.vector.tensor_add(out=pre_z[:, cols], in0=gi[(GATE_Z, start)][:], in1=ghb[:, z_cols])
             nc.scalar.activation(out=gate_z[:, cols], in_=pre_z[:, cols], func=ACT.Sigmoid)
+            nc.gpsimd.tensor_mul(out=z_h[:, cols], in0=gate_z[:, cols], in1=h_sb[:, cols])
+        for start, width in CHUNKS:
+            cols = slice(start, start + width)
             nc.scalar.activation(
                 out=one_minus_z[:, cols], in_=pre_z[:, cols], func=ACT.Sigmoid, scale=-1.0
             )
-            nc.gpsimd.tensor_mul(out=z_h[:, cols], in0=gate_z[:, cols], in1=h_sb[:, cols])
 
         for start, width in CHUNKS:
             cols = slice(start, start + width)
-            n_cols = slice(2 * L + start, 2 * L + start + width)
-            nc.vector.tensor_mul(out=pre_n[:, cols], in0=gate_r[:, cols], in1=gh_sb[:, n_cols])
             nc.vector.tensor_add(
-                out=pre_n[:, cols], in0=bias(2 * L + start, width), in1=pre_n[:, cols]
+                out=gi_b_n[:, cols], in0=gi[(GATE_N, start)][:], in1=bias_n[:, cols]
             )
-            nc.vector.tensor_add(out=pre_n[:, cols], in0=gi[(GATE_N, start)][:], in1=pre_n[:, cols])
+            nc.vector.tensor_mul(out=pre_n[:, cols], in0=gate_r[:, cols], in1=gh_sb[GATE_N][:, cols])
+            nc.vector.tensor_add(out=pre_n[:, cols], in0=pre_n[:, cols], in1=gi_b_n[:, cols])
             nc.scalar.activation(out=gate_n[:, cols], in_=pre_n[:, cols], func=ACT.Tanh)
 
         for start, width in CHUNKS:

@@ -43,7 +43,8 @@ def tile_grucellstack_pa_s_kernel(tc, x, h0, gh0, w_words, w_scales, b_ih0, out)
         bias_rows = keep.tile([P, P], F32)
         nc.vector.memset(bias_rows[:], 0.0)
         w_planes = keep.tile([P, PASSES, GATES * L], U8, align_bytes=64)
-        nc.vector.memset(w_planes[:].rearrange("p g n -> p (g n)").bitcast(I32), 0)
+        nc.vector.memset(w_planes[:, 0, :].bitcast(I32), 0)
+        nc.gpsimd.memset(w_planes[:, 1, :].bitcast(F32), 0.0)
         idle_work = keep.tile([P, P], F32)
         nc.gpsimd.memset(idle_work[:], 0.0)
         warm = keep.tile([P, 1], F32)
@@ -74,14 +75,14 @@ def tile_grucellstack_pa_s_kernel(tc, x, h0, gh0, w_words, w_scales, b_ih0, out)
             gh_sb[gate] = keep.tile([P, L], BF16, name="gh_sb%d" % gate)
             nc.sync.dma_start(out=gh_sb[gate][:], in_=gh0[:, L * gate : L * (gate + 1)])
 
-        load_gh(GATE_R)
-        load_words(GATE_R)
         scale_rows = w_scales.rearrange("g q n -> q g n")
         for r in range(4):
             nc.sync.dma_start(
                 out=w_planes[r:P:32, :, :].bitcast(I32),
                 in_=scale_rows[r:16:4, :, :].bitcast(I32),
             )
+        load_words(GATE_R)
+        load_gh(GATE_R)
         load_words(GATE_Z)
         load_gh(GATE_Z)
         load_words(GATE_N)

@@ -40,15 +40,15 @@ def tile_grucellstack_pa_s_kernel(tc, x, h0, gh0, w_words, w_scales, b_ih0, out)
         keep = ctx.enter_context(tc.tile_pool(name="keep", bufs=1))
         bias_psum = ctx.enter_context(tc.psum_pool(name="bias_psum", bufs=1))
 
+        idle_work = keep.tile([P, P], F32)
+        nc.vector.memset(idle_work[:], 0.0)
+        warm = keep.tile([P, 1], F32)
+        nc.vector.memset(warm[:], 0.0)
         bias_rows = keep.tile([P, P], F32)
         nc.vector.memset(bias_rows[:], 0.0)
         w_planes = keep.tile([P, PASSES, GATES * L], U8, align_bytes=64)
         nc.vector.memset(w_planes[:, 0, :].bitcast(I32), 0)
         nc.gpsimd.memset(w_planes[:, 1, :].bitcast(F32), 0.0)
-        idle_work = keep.tile([P, P], F32)
-        nc.gpsimd.memset(idle_work[:], 0.0)
-        warm = keep.tile([P, 1], F32)
-        nc.gpsimd.memset(warm[:], 0.0)
         identity = keep.tile([P, P], F32)
         make_identity(nc, identity[:])
         nc.scalar.activation(out=warm[:], in_=warm[:], func=ACT.Sigmoid)
@@ -83,9 +83,9 @@ def tile_grucellstack_pa_s_kernel(tc, x, h0, gh0, w_words, w_scales, b_ih0, out)
             )
         load_words(GATE_R)
         load_gh(GATE_R)
-        load_words(GATE_Z)
         load_gh(GATE_Z)
         load_words(GATE_N)
+        load_words(GATE_Z)
         load_gh(GATE_N)
         h_sb = keep.tile([P, L], BF16)
         nc.sync.dma_start(out=h_sb[:], in_=h0)
@@ -102,14 +102,15 @@ def tile_grucellstack_pa_s_kernel(tc, x, h0, gh0, w_words, w_scales, b_ih0, out)
                 )
             x_words = x_sb[:].bitcast(F32)
             x_t = {}
+            bias_t = head_psum.tile([P, P], F32)
             for g in range(PASSES):
                 x_t[g] = head_psum.tile([P, 2, P], F32, name="x_t%d" % g)
                 for u in range(2):
                     nc.tensor.transpose(
                         x_t[g][:, u, :], x_words[:, 256 * g + u : 256 * (g + 1) : 2], identity[:]
                     )
-            bias_t = head_psum.tile([P, P], F32)
-            nc.tensor.transpose(bias_t[:], bias_rows[:], identity[:])
+                if g == 0:
+                    nc.tensor.transpose(bias_t[:], bias_rows[:], identity[:])
             nc.vector.tensor_copy(out=bias_cols[:], in_=bias_t[:, 0 : BIAS_BANKS * PER_BANK])
             for g in range(PASSES):
                 pairs = grouped[:, g].rearrange("p b t -> p (b t)").bitcast(F32)
@@ -165,8 +166,8 @@ def tile_grucellstack_pa_s_kernel(tc, x, h0, gh0, w_words, w_scales, b_ih0, out)
         spread_bias(0)
         spread_bias(1)
         multiply(GATE_R)
-        multiply(GATE_Z)
         multiply(GATE_N)
+        multiply(GATE_Z)
 
         ghb = keep.tile([P, 2 * L], F32)
         bias_n = keep.tile([P, L], BF16)
@@ -189,38 +190,70 @@ def tile_grucellstack_pa_s_kernel(tc, x, h0, gh0, w_words, w_scales, b_ih0, out)
                 in1=gh_sb[gate][:, start : start + width],
             )
 
+        def cols_of(chunk):
+            start, width = CHUNKS[chunk]
+            return slice(start, start + width)
+
+        def add_gi(out_tile, gate, chunk, other):
+            nc.vector.tensor_add(
+                out=out_tile[:, cols_of(chunk)],
+                in0=gi[(gate, CHUNKS[chunk][0])][:],
+                in1=other,
+            )
+
+        def pre_r_of(chunk):
+            add_gi(pre_r, GATE_R, chunk, ghb[:, cols_of(chunk)])
+
+        def pre_z_of(chunk):
+            start, width = CHUNKS[chunk]
+            add_gi(pre_z, GATE_Z, chunk, ghb[:, L + start : L + start + width])
+
+        def gi_b_n_of(chunk):
+            add_gi(gi_b_n, GATE_N, chunk, bias_n[:, cols_of(chunk)])
+
+        def product(out_tile, a, b, chunk):
+            cols = cols_of(chunk)
+            nc.vector.tensor_mul(out=out_tile[:, cols], in0=a[:, cols], in1=b[:, cols])
+
+        def total(out_tile, a, b, chunk):
+            cols = cols_of(chunk)
+            nc.vector.tensor_add(out=out_tile[:, cols], in0=a[:, cols], in1=b[:, cols])
+
+        def act(out_tile, in_tile, func, chunk, scale=1.0):
+            cols = cols_of(chunk)
+            nc.scalar.activation(out=out_tile[:, cols], in_=in_tile[:, cols], func=func, scale=scale)
+
+        A, B = 0, 1
+        r_gh = keep.tile([P, L], F32)
+        part_n = keep.tile([P, L], F32)
+
         add_bias_to_gh(GATE_R, 0, L)
         nc.scalar.copy(out=bias_n[:], in_=bias(GATE_N * L, L))
-        for start, width in CHUNKS:
-            cols = slice(start, start + width)
-            nc.vector.tensor_add(out=pre_r[:, cols], in0=gi[(GATE_R, start)][:], in1=ghb[:, cols])
-            nc.scalar.activation(out=gate_r[:, cols], in_=pre_r[:, cols], func=ACT.Sigmoid)
-
+        pre_r_of(A)
+        act(gate_r, pre_r, ACT.Sigmoid, A)
+        pre_r_of(B)
+        act(gate_r, pre_r, ACT.Sigmoid, B)
         add_bias_to_gh(GATE_Z, 0, BANK_BIAS - L)
         add_bias_to_gh(GATE_Z, BANK_BIAS - L, 2 * L - BANK_BIAS)
-        for start, width in CHUNKS:
-            cols = slice(start, start + width)
-            z_cols = slice(L + start, L + start + width)
-            nc.vector.tensor_add(out=pre_z[:, cols], in0=gi[(GATE_Z, start)][:], in1=ghb[:, z_cols])
-            nc.scalar.activation(out=gate_z[:, cols], in_=pre_z[:, cols], func=ACT.Sigmoid)
-            nc.gpsimd.tensor_mul(out=z_h[:, cols], in0=gate_z[:, cols], in1=h_sb[:, cols])
-        for start, width in CHUNKS:
-            cols = slice(start, start + width)
-            nc.scalar.activation(
-                out=one_minus_z[:, cols], in_=pre_z[:, cols], func=ACT.Sigmoid, scale=-1.0
-            )
-
-        for start, width in CHUNKS:
-            cols = slice(start, start + width)
-            nc.vector.tensor_add(
-                out=gi_b_n[:, cols], in0=gi[(GATE_N, start)][:], in1=bias_n[:, cols]
-            )
-            nc.vector.tensor_mul(out=pre_n[:, cols], in0=gate_r[:, cols], in1=gh_sb[GATE_N][:, cols])
-            nc.vector.tensor_add(out=pre_n[:, cols], in0=pre_n[:, cols], in1=gi_b_n[:, cols])
-            nc.scalar.activation(out=gate_n[:, cols], in_=pre_n[:, cols], func=ACT.Tanh)
-
-        for start, width in CHUNKS:
-            cols = slice(start, start + width)
-            nc.vector.tensor_mul(out=blend[:, cols], in0=one_minus_z[:, cols], in1=gate_n[:, cols])
-            nc.vector.tensor_add(out=blend[:, cols], in0=blend[:, cols], in1=z_h[:, cols])
-            nc.sync.dma_start(out=out[:, cols], in_=blend[:, cols])
+        gi_b_n_of(A)
+        pre_z_of(A)
+        act(gate_z, pre_z, ACT.Sigmoid, A)
+        act(one_minus_z, pre_z, ACT.Sigmoid, A, scale=-1.0)
+        product(r_gh, gate_r, gh_sb[GATE_N], A)
+        pre_z_of(B)
+        act(gate_z, pre_z, ACT.Sigmoid, B)
+        act(one_minus_z, pre_z, ACT.Sigmoid, B, scale=-1.0)
+        gi_b_n_of(B)
+        total(pre_n, r_gh, gi_b_n, A)
+        act(gate_n, pre_n, ACT.Tanh, A)
+        product(r_gh, gate_r, gh_sb[GATE_N], B)
+        product(z_h, gate_z, h_sb, A)
+        total(pre_n, r_gh, gi_b_n, B)
+        act(gate_n, pre_n, ACT.Tanh, B)
+        product(part_n, one_minus_z, gate_n, A)
+        product(z_h, gate_z, h_sb, B)
+        product(part_n, one_minus_z, gate_n, B)
+        total(blend, part_n, z_h, A)
+        nc.sync.dma_start(out=out[:, cols_of(A)], in_=blend[:, cols_of(A)])
+        total(blend, part_n, z_h, B)
+        nc.sync.dma_start(out=out[:, cols_of(B)], in_=blend[:, cols_of(B)])

@@ -26,7 +26,7 @@ BIAS_BANKS = 2
 BIAS_ROWS = BIAS_BANKS * PER_BANK
 ROW_WORDS = GATES * L // (2 * BIAS_ROWS)
 BANK_BIAS = 2 * ROW_WORDS * PER_BANK
-IDLE_MATMULS = 4
+IDLE_WIDTHS = (128, 128, 128, 64)
 
 CHUNKS = ((0, 512), (512, 128))
 
@@ -41,9 +41,9 @@ def tile_grucellstack_pa_s_kernel(tc, x, h0, gh0, w_words, w_scales, b_ih0, out)
         bias_psum = ctx.enter_context(tc.psum_pool(name="bias_psum", bufs=1))
 
         idle_work = keep.tile([P, P], F32)
-        nc.vector.memset(idle_work[:], 0.0)
+        nc.gpsimd.memset(idle_work[:], 0.0)
         warm = keep.tile([P, 1], F32)
-        nc.vector.memset(warm[:], 0.0)
+        nc.gpsimd.memset(warm[:], 0.0)
         bias_rows = keep.tile([P, P], F32)
         nc.vector.memset(bias_rows[:], 0.0)
         w_planes = keep.tile([P, PASSES, GATES * L], U8, align_bytes=64)
@@ -96,9 +96,13 @@ def tile_grucellstack_pa_s_kernel(tc, x, h0, gh0, w_words, w_scales, b_ih0, out)
         x_planes = keep.tile([P, PASSES, P], U8, align_bytes=64)
         with tc.psum_pool(name="head_psum", bufs=1) as head_psum:
             idle_out = head_psum.tile([P, P], F32)
-            for i in range(IDLE_MATMULS):
+            for width in IDLE_WIDTHS:
                 nc.tensor.matmul(
-                    out=idle_out[:], lhsT=idle_work[:], rhs=idle_work[:], start=True, stop=True
+                    out=idle_out[:, 0:width],
+                    lhsT=idle_work[:],
+                    rhs=idle_work[:, 0:width],
+                    start=True,
+                    stop=True,
                 )
             x_words = x_sb[:].bitcast(F32)
             x_t = {}
@@ -229,11 +233,11 @@ def tile_grucellstack_pa_s_kernel(tc, x, h0, gh0, w_words, w_scales, b_ih0, out)
 
         add_bias_to_gh(GATE_R, 0, L)
         nc.scalar.copy(out=bias_n[:], in_=bias(GATE_N * L, L))
+        add_bias_to_gh(GATE_Z, 0, BANK_BIAS - L)
         pre_r_of(A)
         act(gate_r, pre_r, ACT.Sigmoid, A)
         pre_r_of(B)
         act(gate_r, pre_r, ACT.Sigmoid, B)
-        add_bias_to_gh(GATE_Z, 0, BANK_BIAS - L)
         add_bias_to_gh(GATE_Z, BANK_BIAS - L, 2 * L - BANK_BIAS)
         gi_b_n_of(A)
         pre_z_of(A)

@@ -41,15 +41,17 @@ def tile_grucellstack_pa_s_kernel(tc, x, h0, gh0, w_words, w_scales, b_ih0, out)
         bias_psum = ctx.enter_context(tc.psum_pool(name="bias_psum", bufs=1))
 
         idle_work = keep.tile([P, P], F32)
-        nc.gpsimd.memset(idle_work[:], 0.0)
+        nc.vector.memset(idle_work[:], 0.0)
         warm = keep.tile([P, 1], F32)
-        nc.gpsimd.memset(warm[:], 0.0)
+        nc.vector.memset(warm[:], 0.0)
         bias_rows = keep.tile([P, P], F32)
         nc.vector.memset(bias_rows[:], 0.0)
-        w_planes = keep.tile([P, PASSES, GATES * L], U8, align_bytes=64)
-        nc.vector.memset(w_planes[:, 0, :].bitcast(I32), 0)
-        nc.gpsimd.memset(w_planes[:, 1, :].bitcast(F32), 0.0)
+        planes_r = keep.tile([P, PASSES, L], U8, align_bytes=64)
+        nc.vector.memset(planes_r[:].rearrange("p g n -> p (g n)").bitcast(I32), 0)
         identity = keep.tile([P, P], F32)
+        nc.vector.memset(identity[:], 0.0)
+        planes_zn = keep.tile([P, PASSES, 2 * L], U8, align_bytes=64)
+        nc.vector.memset(planes_zn[:].rearrange("p g n -> p (g n)").bitcast(I32), 0)
         make_identity(nc, identity[:])
         nc.scalar.activation(out=warm[:], in_=warm[:], func=ACT.Sigmoid)
 
@@ -76,13 +78,18 @@ def tile_grucellstack_pa_s_kernel(tc, x, h0, gh0, w_words, w_scales, b_ih0, out)
             nc.sync.dma_start(out=gh_sb[gate][:], in_=gh0[:, L * gate : L * (gate + 1)])
 
         scale_rows = w_scales.rearrange("g q n -> q g n")
-        for r in range(4):
-            nc.sync.dma_start(
-                out=w_planes[r:P:32, :, :].bitcast(I32),
-                in_=scale_rows[r:16:4, :, :].bitcast(I32),
-            )
+
+        def load_scales(planes, first, width):
+            for r in range(4):
+                nc.sync.dma_start(
+                    out=planes[r:P:32, :, :].bitcast(I32),
+                    in_=scale_rows[r:16:4, :, first : first + width].bitcast(I32),
+                )
+
+        load_scales(planes_r, 0, L)
         load_words(GATE_R)
         load_gh(GATE_R)
+        load_scales(planes_zn, L, 2 * L)
         load_gh(GATE_Z)
         load_words(GATE_N)
         load_words(GATE_Z)
@@ -156,13 +163,13 @@ def tile_grucellstack_pa_s_kernel(tc, x, h0, gh0, w_words, w_scales, b_ih0, out)
                 gi[(gate, start)] = gi_psum.tile([P, width], F32, name="gi%d_%d" % (gate, start))
             for g in range(PASSES):
                 for start, width in CHUNKS:
-                    first = gate * L + start
+                    planes, first = (planes_r, start) if gate == GATE_R else (planes_zn, (gate - 1) * L + start)
                     nc.tensor.matmul_mx(
                         out=gi[(gate, start)][:],
                         lhsT=x_codes[:, g, :].bitcast(FP8X4),
                         lhsT_scale=x_planes[:, g, :],
                         rhs=w_sb[gate][:, g, 2 * start : 2 * (start + width)].bitcast(FP4X4),
-                        rhs_scale=w_planes[:, g, first : first + width],
+                        rhs_scale=planes[:, g, first : first + width],
                         start=(g == 0),
                         stop=(g == PASSES - 1),
                     )

@@ -264,7 +264,7 @@ def tile_grucellstack_pa_s_kernel(tc, x, h0, gh0, w_words, w_scales, b_ih0, out)
         product(part_n, one_minus_z, gate_n, A)
         product(z_h, gate_z, h_sb, B)
         product(part_n, one_minus_z, gate_n, B)
-        total(blend, part_n, z_h, A)
-        nc.sync.dma_start(out=out[:, cols_of(A)], in_=blend[:, cols_of(A)])
-        total(blend, part_n, z_h, B)
-        nc.sync.dma_start(out=out[:, cols_of(B)], in_=blend[:, cols_of(B)])
+        for first, width in ((0, 256), (256, 256), (512, 128)):
+            cols = slice(first, first + width)
+            nc.vector.tensor_add(out=blend[:, cols], in0=part_n[:, cols], in1=z_h[:, cols])
+            nc.sync.dma_start(out=out[:, cols], in_=blend[:, cols])

@@ -11,6 +11,7 @@ U8 = mybir.dt.uint8
 FP8X4 = mybir.dt.float8_e4m3fn_x4
 FP4X4 = mybir.dt.float4_e2m1fn_x4
 ACT = mybir.ActivationFunctionType
+ALU = mybir.AluOpType
 
 P = 128
 PACK = 4
@@ -188,7 +189,6 @@ def tile_grucellstack_pa_s_kernel(tc, x, h0, gh0, w_words, w_scales, b_ih0, out)
         pre_n = keep.tile([P, L], F32)
         gate_r = keep.tile([P, L], F32)
         gate_z = keep.tile([P, L], F32)
-        one_minus_z = keep.tile([P, L], F32)
         gate_n = keep.tile([P, L], F32)
         z_h = keep.tile([P, L], F32)
         blend = keep.tile([P, L], F32)
@@ -241,30 +241,39 @@ def tile_grucellstack_pa_s_kernel(tc, x, h0, gh0, w_words, w_scales, b_ih0, out)
         add_bias_to_gh(GATE_R, 0, L)
         nc.scalar.copy(out=bias_n[:], in_=bias(GATE_N * L, L))
         add_bias_to_gh(GATE_Z, 0, BANK_BIAS - L)
+        def minus_part_n_of(chunk):
+            cols = cols_of(chunk)
+            nc.vector.scalar_tensor_tensor(
+                out=part_n[:, cols],
+                in0=gate_z[:, cols],
+                scalar=1.0,
+                in1=gate_n[:, cols],
+                op0=ALU.subtract,
+                op1=ALU.mult,
+            )
+
         pre_r_of(A)
         act(gate_r, pre_r, ACT.Sigmoid, A)
         pre_r_of(B)
         act(gate_r, pre_r, ACT.Sigmoid, B)
         add_bias_to_gh(GATE_Z, BANK_BIAS - L, 2 * L - BANK_BIAS)
         gi_b_n_of(A)
+        product(r_gh, gate_r, gh_sb[GATE_N], A)
         pre_z_of(A)
         act(gate_z, pre_z, ACT.Sigmoid, A)
-        act(one_minus_z, pre_z, ACT.Sigmoid, A, scale=-1.0)
-        product(r_gh, gate_r, gh_sb[GATE_N], A)
-        pre_z_of(B)
-        act(gate_z, pre_z, ACT.Sigmoid, B)
-        act(one_minus_z, pre_z, ACT.Sigmoid, B, scale=-1.0)
-        gi_b_n_of(B)
         total(pre_n, r_gh, gi_b_n, A)
         act(gate_n, pre_n, ACT.Tanh, A)
+        pre_z_of(B)
+        act(gate_z, pre_z, ACT.Sigmoid, B)
+        gi_b_n_of(B)
         product(r_gh, gate_r, gh_sb[GATE_N], B)
         product(z_h, gate_z, h_sb, A)
         total(pre_n, r_gh, gi_b_n, B)
         act(gate_n, pre_n, ACT.Tanh, B)
-        product(part_n, one_minus_z, gate_n, A)
+        minus_part_n_of(A)
         product(z_h, gate_z, h_sb, B)
-        product(part_n, one_minus_z, gate_n, B)
+        minus_part_n_of(B)
         for first, width in ((0, 256), (256, 256), (512, 128)):
             cols = slice(first, first + width)
-            nc.vector.tensor_add(out=blend[:, cols], in0=part_n[:, cols], in1=z_h[:, cols])
+            nc.vector.tensor_sub(out=blend[:, cols], in0=z_h[:, cols], in1=part_n[:, cols])
             nc.sync.dma_start(out=out[:, cols], in_=blend[:, cols])

@@ -20,16 +20,11 @@ PASSES = K // (P * PACK)
 L = 640
 GATE_R, GATE_Z, GATE_N = 0, 1, 2
 GATES = 3
-BANK_F32 = 512
-BANK_BF16 = 2 * BANK_F32
-PER_BANK = BANK_F32 // P
-BIAS_BANKS = 2
-BIAS_ROWS = BIAS_BANKS * PER_BANK
-ROW_WORDS = GATES * L // (2 * BIAS_ROWS)
-BANK_BIAS = 2 * ROW_WORDS * PER_BANK
-IDLE_WIDTHS = (128, 128, 128, 64)
+CHUNKS = L // P
+IDLE_WIDTHS = (128, 128, 128)
 
-CHUNKS = ((0, 512), (512, 128))
+PIECES = ((0, 3), (3, 2))
+Z_PIECES = ((0, 512), (512, 128))
 
 FLOPS = 2 * P * K * GATES * L
 
@@ -39,33 +34,36 @@ def tile_grucellstack_pa_s_kernel(tc, x, h0, gh0, w_words, w_scales, b_ih0, out)
     with ExitStack() as ctx:
         ctx.enter_context(tc.manual_schedule())
         keep = ctx.enter_context(tc.tile_pool(name="keep", bufs=1))
-        bias_psum = ctx.enter_context(tc.psum_pool(name="bias_psum", bufs=1))
+        psum = ctx.enter_context(tc.psum_pool(name="psum", bufs=1))
 
         idle_work = keep.tile([P, P], F32)
-        nc.vector.memset(idle_work[:], 0.0)
+        bias_rows = keep.tile([P, P], BF16)
         warm = keep.tile([P, 1], F32)
-        nc.vector.memset(warm[:], 0.0)
-        bias_rows = keep.tile([P, P], F32)
-        nc.vector.memset(bias_rows[:], 0.0)
-        planes_r = keep.tile([P, PASSES, L], U8, align_bytes=64)
-        nc.vector.memset(planes_r[:].rearrange("p g n -> p (g n)").bitcast(I32), 0)
+        planes = keep.tile([P, PASSES, GATES * L], U8, align_bytes=64)
         identity = keep.tile([P, P], F32)
-        nc.vector.memset(identity[:], 0.0)
-        planes_zn = keep.tile([P, PASSES, 2 * L], U8, align_bytes=64)
-        nc.vector.memset(planes_zn[:].rearrange("p g n -> p (g n)").bitcast(I32), 0)
+        identity_bf = keep.tile([P, P], BF16)
+        gh_sb = {}
+        for gate in range(GATES):
+            gh_sb[gate] = keep.tile([P, L], BF16, name="gh_sb%d" % gate)
+        nc.vector.memset(idle_work[:], 0.0)
+        nc.vector.memset(warm[:], 0.0)
+        nc.vector.memset(bias_rows[:], 0.0)
         make_identity(nc, identity[:])
-        nc.scalar.activation(out=warm[:], in_=warm[:], func=ACT.Sigmoid)
+        nc.gpsimd.dma_start(out=gh_sb[GATE_Z][:], in_=gh0[:, L * GATE_Z : L * (GATE_Z + 1)])
 
         x_sb = keep.tile([P, K], BF16)
         nc.sync.dma_start(out=x_sb[:], in_=x)
-        nc.sync.dma_start(
-            out=bias_rows[:].bitcast(BF16)[0:BIAS_ROWS, 0 : 2 * ROW_WORDS],
-            in_=b_ih0.rearrange("(c j) -> c j", j=2 * ROW_WORDS),
-        )
+        nc.sync.dma_start(out=gh_sb[GATE_R][:], in_=gh0[:, L * GATE_R : L * (GATE_R + 1)])
+        nc.scalar.activation(out=warm[:], in_=warm[:], func=ACT.Sigmoid)
+
+        scale_rows = w_scales.rearrange("g q n -> q g n")
+        for r in range(4):
+            nc.sync.dma_start(
+                out=planes[r:P:32, :, :].bitcast(I32), in_=scale_rows[r:16:4, :, :].bitcast(I32)
+            )
 
         word_rows = w_words.rearrange("g p n -> p g n")
         w_sb = {}
-        gh_sb = {}
 
         def load_words(gate):
             w_sb[gate] = keep.tile([P, PASSES, 2 * L], U8, align_bytes=64, name="w_sb%d" % gate)
@@ -75,205 +73,220 @@ def tile_grucellstack_pa_s_kernel(tc, x, h0, gh0, w_words, w_scales, b_ih0, out)
             )
 
         def load_gh(gate):
-            gh_sb[gate] = keep.tile([P, L], BF16, name="gh_sb%d" % gate)
             nc.sync.dma_start(out=gh_sb[gate][:], in_=gh0[:, L * gate : L * (gate + 1)])
 
-        scale_rows = w_scales.rearrange("g q n -> q g n")
-
-        def load_scales(planes, first, width):
-            for r in range(4):
-                nc.sync.dma_start(
-                    out=planes[r:P:32, :, :].bitcast(I32),
-                    in_=scale_rows[r:16:4, :, first : first + width].bitcast(I32),
-                )
-
-        load_scales(planes_r, 0, L)
+        nc.sync.dma_start(
+            out=bias_rows[0 : GATES * CHUNKS, :], in_=b_ih0.rearrange("(c p) -> c p", p=P)
+        )
         load_words(GATE_R)
-        load_gh(GATE_R)
-        load_scales(planes_zn, L, 2 * L)
-        load_gh(GATE_Z)
-        load_words(GATE_N)
         load_words(GATE_Z)
         load_gh(GATE_N)
+        load_words(GATE_N)
         h_sb = keep.tile([P, L], BF16)
         nc.sync.dma_start(out=h_sb[:], in_=h0)
 
-        bias_cols = keep.tile([P, BIAS_BANKS * PER_BANK], F32)
+        bias_cols = keep.tile([P, GATES * CHUNKS], F32)
         grouped = keep.tile([P, PASSES, P, PACK], BF16, align_bytes=64)
         x_codes = keep.tile([P, PASSES, P], U32, align_bytes=64)
         x_planes = keep.tile([P, PASSES, P], U8, align_bytes=64)
-        with tc.psum_pool(name="head_psum", bufs=1) as head_psum:
-            idle_out = head_psum.tile([P, P], F32)
-            for width in IDLE_WIDTHS:
-                nc.tensor.matmul(
-                    out=idle_out[:, 0:width],
-                    lhsT=idle_work[:],
-                    rhs=idle_work[:, 0:width],
-                    start=True,
-                    stop=True,
-                )
-            x_words = x_sb[:].bitcast(F32)
-            x_t = {}
-            bias_t = head_psum.tile([P, P], F32)
-            for g in range(PASSES):
-                x_t[g] = head_psum.tile([P, 2, P], F32, name="x_t%d" % g)
-                for u in range(2):
-                    nc.tensor.transpose(
-                        x_t[g][:, u, :], x_words[:, 256 * g + u : 256 * (g + 1) : 2], identity[:]
-                    )
-                if g == 0:
-                    nc.tensor.transpose(bias_t[:], bias_rows[:], identity[:])
-            nc.vector.tensor_copy(out=bias_cols[:], in_=bias_t[:, 0 : BIAS_BANKS * PER_BANK])
-            for g in range(PASSES):
-                pairs = grouped[:, g].rearrange("p b t -> p (b t)").bitcast(F32)
-                nc.scalar.copy(
-                    out=pairs.rearrange("p (b u) -> p b u", u=2),
-                    in_=x_t[g][:].rearrange("p u b -> p b u"),
-                )
-            for g in range(PASSES):
-                nc.vector.quantize_mx(
-                    out=x_codes[:, g, :].bitcast(FP8X4),
-                    scales=x_planes[:, g, :],
-                    in_=grouped[:, g].rearrange("p b t -> p (b t)"),
-                )
 
-        bias_banks = [
-            bias_psum.tile([P, BANK_F32], F32, name="bias_bank%d" % i) for i in range(BIAS_BANKS)
-        ]
-
-        def spread_bias(bank):
-            for i in range(PER_BANK):
-                c = PER_BANK * bank + i
+        idle_out = psum.tile([P, P], F32, tag="z1")
+        for width in IDLE_WIDTHS:
+            nc.tensor.matmul(
+                out=idle_out[:, 0:width],
+                lhsT=idle_work[:],
+                rhs=idle_work[:, 0:width],
+                start=True,
+                stop=True,
+            )
+        x_words = x_sb[:].bitcast(F32)
+        x_t = {}
+        for g in range(PASSES):
+            x_t[g] = psum.tile([P, 2, P], F32, name="x_t%d" % g, tag="t%d" % g)
+            for u in range(2):
                 nc.tensor.transpose(
-                    bias_banks[bank][:, ROW_WORDS * i : ROW_WORDS * i + P],
-                    bias_cols[:, c : c + 1].to_broadcast([P, P]),
-                    identity[:],
+                    x_t[g][:, u, :], x_words[:, 256 * g + u : 256 * (g + 1) : 2], identity[:]
+                )
+        nc.vector.tensor_copy(out=identity_bf[:], in_=identity[:])
+        bias_t = psum.tile([P, P], BF16, tag="z1")
+        nc.tensor.transpose(bias_t[:], bias_rows[:], identity_bf[:])
+        nc.vector.tensor_copy(out=bias_cols[:], in_=bias_t[:, 0 : GATES * CHUNKS])
+        for g in range(PASSES):
+            pairs = grouped[:, g].rearrange("p b t -> p (b t)").bitcast(F32)
+            nc.scalar.copy(
+                out=pairs.rearrange("p (b u) -> p b u", u=2),
+                in_=x_t[g][:].rearrange("p u b -> p b u"),
+            )
+        for g in range(PASSES):
+            nc.vector.quantize_mx(
+                out=x_codes[:, g, :].bitcast(FP8X4),
+                scales=x_planes[:, g, :],
+                in_=grouped[:, g].rearrange("p b t -> p (b t)"),
+            )
+
+        gh_t = {}
+
+        def turn_gh(gate, tag):
+            gh_t[gate] = psum.tile([P, CHUNKS, P], BF16, name="gh_t%d" % gate, tag=tag)
+            for c in range(CHUNKS):
+                nc.tensor.transpose(
+                    gh_t[gate][:, c, :], gh_sb[gate][:, P * c : P * (c + 1)], identity_bf[:]
                 )
 
-        def bias(first, width):
-            bank = first // BANK_BIAS
-            at = first - bank * BANK_BIAS
-            assert at + width <= BANK_BIAS
-            return bias_banks[bank][:].bitcast(BF16)[:, at : at + width]
-
-        gi_psum = ctx.enter_context(tc.psum_pool(name="gi_psum", bufs=1, reuse_waits="tile"))
         gi = {}
 
-        def multiply(gate):
-            for start, width in CHUNKS:
-                gi[(gate, start)] = gi_psum.tile([P, width], F32, name="gi%d_%d" % (gate, start))
-            for g in range(PASSES):
-                for start, width in CHUNKS:
-                    planes, first = (planes_r, start) if gate == GATE_R else (planes_zn, (gate - 1) * L + start)
+        def multiply(gate, tags):
+            for (first, count), tag in zip(PIECES, tags):
+                piece = psum.tile([P, count, P], F32, name="gi%d_%d" % (gate, first), tag=tag)
+                gi[(gate, first)] = piece
+                for c in range(first, first + count):
+                    for g in range(PASSES):
+                        nc.tensor.matmul_mx(
+                            out=piece[:, c - first, :],
+                            lhsT=w_sb[gate][:, g, 2 * P * c : 2 * P * (c + 1)].bitcast(FP4X4),
+                            lhsT_scale=planes[:, g, gate * L + P * c : gate * L + P * (c + 1)],
+                            rhs=x_codes[:, g, :].bitcast(FP8X4),
+                            rhs_scale=x_planes[:, g, :],
+                            start=(g == 0),
+                            stop=(g == PASSES - 1),
+                        )
+
+        def multiply_z():
+            for (first, width), tag in zip(Z_PIECES, ("z0", "z1")):
+                piece = psum.tile([P, width], F32, name="gi_z%d" % first, tag=tag)
+                gi[(GATE_Z, first)] = piece
+                for g in range(PASSES):
                     nc.tensor.matmul_mx(
-                        out=gi[(gate, start)][:],
+                        out=piece[:],
                         lhsT=x_codes[:, g, :].bitcast(FP8X4),
                         lhsT_scale=x_planes[:, g, :],
-                        rhs=w_sb[gate][:, g, 2 * start : 2 * (start + width)].bitcast(FP4X4),
-                        rhs_scale=planes[:, g, first : first + width],
+                        rhs=w_sb[GATE_Z][:, g, 2 * first : 2 * (first + width)].bitcast(FP4X4),
+                        rhs_scale=planes[:, g, L + first : L + first + width],
                         start=(g == 0),
                         stop=(g == PASSES - 1),
                     )
 
-        spread_bias(0)
-        spread_bias(1)
-        multiply(GATE_R)
-        multiply(GATE_N)
-        multiply(GATE_Z)
+        turn_gh(GATE_R, "z0")
 
-        ghb = keep.tile([P, 2 * L], F32)
-        bias_n = keep.tile([P, L], BF16)
-        pre_r = keep.tile([P, L], F32)
+        bias_z = {}
+        for (first, width), tag in zip(Z_PIECES, ("n0", "n1")):
+            bias_z[first] = psum.tile([P, width], F32, name="bias_z%d" % first, tag=tag)
+            for c in range(width // P):
+                col = GATE_Z * CHUNKS + first // P + c
+                nc.tensor.transpose(
+                    bias_z[first][:, P * c : P * (c + 1)],
+                    bias_cols[:, col : col + 1].to_broadcast([P, P]),
+                    identity[:],
+                )
+
+        gh_r_t = keep.tile([P, CHUNKS, P], BF16)
+        ghb_z = keep.tile([P, L], F32)
+
+        nc.vector.tensor_copy(out=gh_r_t[:], in_=gh_t[GATE_R][:])
+        for first, width in Z_PIECES:
+            cols = slice(first, first + width)
+            nc.vector.tensor_add(out=ghb_z[:, cols], in0=bias_z[first][:], in1=gh_sb[GATE_Z][:, cols])
+        multiply(GATE_R, ("r0", "r1"))
+        multiply_z()
+        turn_gh(GATE_N, "t0")
+        multiply(GATE_N, ("n0", "n1"))
+
+        pre_r = keep.tile([P, CHUNKS, P], F32)
+        pre_n = keep.tile([P, CHUNKS, P], F32)
         pre_z = keep.tile([P, L], F32)
-        gi_b_n = keep.tile([P, L], F32)
-        pre_n = keep.tile([P, L], F32)
-        gate_r = keep.tile([P, L], F32)
+        gate_r = keep.tile([P, CHUNKS, P], F32)
+        gate_n = keep.tile([P, CHUNKS, P], F32)
         gate_z = keep.tile([P, L], F32)
-        gate_n = keep.tile([P, L], F32)
+        r_gh = keep.tile([P, CHUNKS, P], F32)
+        part_n = keep.tile([P, L], F32)
         z_h = keep.tile([P, L], F32)
         blend = keep.tile([P, L], F32)
 
-        def add_bias_to_gh(gate, start, width):
-            first = gate * L + start
-            nc.vector.tensor_add(
-                out=ghb[:, first : first + width],
-                in0=bias(first, width),
-                in1=gh_sb[gate][:, start : start + width],
-            )
-
-        def cols_of(chunk):
-            start, width = CHUNKS[chunk]
-            return slice(start, start + width)
-
-        def add_gi(out_tile, gate, chunk, other):
-            nc.vector.tensor_add(
-                out=out_tile[:, cols_of(chunk)],
-                in0=gi[(gate, CHUNKS[chunk][0])][:],
-                in1=other,
-            )
-
-        def pre_r_of(chunk):
-            add_gi(pre_r, GATE_R, chunk, ghb[:, cols_of(chunk)])
-
-        def pre_z_of(chunk):
-            start, width = CHUNKS[chunk]
-            add_gi(pre_z, GATE_Z, chunk, ghb[:, L + start : L + start + width])
-
-        def gi_b_n_of(chunk):
-            add_gi(gi_b_n, GATE_N, chunk, bias_n[:, cols_of(chunk)])
-
-        def product(out_tile, a, b, chunk):
-            cols = cols_of(chunk)
-            nc.vector.tensor_mul(out=out_tile[:, cols], in0=a[:, cols], in1=b[:, cols])
-
-        def total(out_tile, a, b, chunk):
-            cols = cols_of(chunk)
-            nc.vector.tensor_add(out=out_tile[:, cols], in0=a[:, cols], in1=b[:, cols])
-
-        def act(out_tile, in_tile, func, chunk, scale=1.0):
-            cols = cols_of(chunk)
-            nc.scalar.activation(out=out_tile[:, cols], in_=in_tile[:, cols], func=func, scale=scale)
-
         A, B = 0, 1
-        r_gh = keep.tile([P, L], F32)
-        part_n = keep.tile([P, L], F32)
 
-        add_bias_to_gh(GATE_R, 0, L)
-        nc.scalar.copy(out=bias_n[:], in_=bias(GATE_N * L, L))
-        add_bias_to_gh(GATE_Z, 0, BANK_BIAS - L)
-        def minus_part_n_of(chunk):
-            cols = cols_of(chunk)
+        def chunks_of(piece):
+            first, count = PIECES[piece]
+            return slice(first, first + count)
+
+        def cols_of(piece):
+            first, count = PIECES[piece]
+            return slice(P * first, P * (first + count))
+
+        def add_gi(out_tile, gate, piece, other):
+            nc.vector.tensor_add(
+                out=out_tile[:, chunks_of(piece), :],
+                in0=gi[(gate, PIECES[piece][0])][:],
+                in1=other[:, chunks_of(piece), :],
+            )
+
+        def act(out_tile, in_tile, gate, func, piece):
+            first, count = PIECES[piece]
+            for c in range(first, first + count):
+                nc.scalar.activation(
+                    out=out_tile[:, c, :],
+                    in_=in_tile[:, c, :],
+                    func=func,
+                    bias=bias_cols[:, gate * CHUNKS + c : gate * CHUNKS + c + 1],
+                )
+
+        def gate_z_of(piece):
+            first, width = Z_PIECES[piece]
+            cols = slice(first, first + width)
+            nc.vector.tensor_add(out=pre_z[:, cols], in0=gi[(GATE_Z, first)][:], in1=ghb_z[:, cols])
+            nc.scalar.activation(out=gate_z[:, cols], in_=pre_z[:, cols], func=ACT.Sigmoid)
+
+        def times_gh_n(piece):
+            nc.vector.tensor_mul(
+                out=r_gh[:, chunks_of(piece), :],
+                in0=gate_r[:, chunks_of(piece), :],
+                in1=gh_t[GATE_N][:, chunks_of(piece), :],
+            )
+
+        n_back = {}
+
+        def turn_back(piece, tag):
+            first, count = PIECES[piece]
+            n_back[piece] = psum.tile([P, count, P], F32, name="n_back%d" % piece, tag=tag)
+            for c in range(first, first + count):
+                nc.tensor.transpose(n_back[piece][:, c - first, :], gate_n[:, c, :], identity[:])
+
+        def times_h(piece):
+            cols = cols_of(piece)
+            nc.vector.tensor_mul(out=z_h[:, cols], in0=gate_z[:, cols], in1=h_sb[:, cols])
+
+        def minus_part_n(piece):
+            cols = cols_of(piece)
             nc.vector.scalar_tensor_tensor(
                 out=part_n[:, cols],
                 in0=gate_z[:, cols],
                 scalar=1.0,
-                in1=gate_n[:, cols],
+                in1=n_back[piece][:].rearrange("p c b -> p (c b)"),
                 op0=ALU.subtract,
                 op1=ALU.mult,
             )
 
-        pre_r_of(A)
-        act(gate_r, pre_r, ACT.Sigmoid, A)
-        pre_r_of(B)
-        act(gate_r, pre_r, ACT.Sigmoid, B)
-        add_bias_to_gh(GATE_Z, BANK_BIAS - L, 2 * L - BANK_BIAS)
-        gi_b_n_of(A)
-        product(r_gh, gate_r, gh_sb[GATE_N], A)
-        pre_z_of(A)
-        act(gate_z, pre_z, ACT.Sigmoid, A)
-        total(pre_n, r_gh, gi_b_n, A)
-        act(gate_n, pre_n, ACT.Tanh, A)
-        pre_z_of(B)
-        act(gate_z, pre_z, ACT.Sigmoid, B)
-        gi_b_n_of(B)
-        product(r_gh, gate_r, gh_sb[GATE_N], B)
-        product(z_h, gate_z, h_sb, A)
-        total(pre_n, r_gh, gi_b_n, B)
-        act(gate_n, pre_n, ACT.Tanh, B)
-        minus_part_n_of(A)
-        product(z_h, gate_z, h_sb, B)
-        minus_part_n_of(B)
-        for first, width in ((0, 256), (256, 256), (512, 128)):
-            cols = slice(first, first + width)
+        def finish(piece):
+            cols = cols_of(piece)
             nc.vector.tensor_sub(out=blend[:, cols], in0=z_h[:, cols], in1=part_n[:, cols])
             nc.sync.dma_start(out=out[:, cols], in_=blend[:, cols])
+
+        add_gi(pre_r, GATE_R, A, gh_r_t)
+        act(gate_r, pre_r, GATE_R, ACT.Sigmoid, A)
+        add_gi(pre_r, GATE_R, B, gh_r_t)
+        act(gate_r, pre_r, GATE_R, ACT.Sigmoid, B)
+        gate_z_of(A)
+        gate_z_of(B)
+        times_gh_n(A)
+        times_gh_n(B)
+        add_gi(pre_n, GATE_N, A, r_gh)
+        act(gate_n, pre_n, GATE_N, ACT.Tanh, A)
+        add_gi(pre_n, GATE_N, B, r_gh)
+        act(gate_n, pre_n, GATE_N, ACT.Tanh, B)
+        times_h(A)
+        times_h(B)
+        turn_back(A, "r0")
+        turn_back(B, "r1")
+        minus_part_n(A)
+        minus_part_n(B)
+        finish(A)
+        finish(B)

@@ -21,7 +21,6 @@ L = 640
 GATE_R, GATE_Z, GATE_N = 0, 1, 2
 GATES = 3
 CHUNKS = L // P
-IDLE_WIDTHS = (128, 128, 128)
 
 PIECES = ((0, 3), (3, 2))
 Z_PIECES = ((0, 512), (512, 128))
@@ -39,7 +38,8 @@ def tile_grucellstack_pa_s_kernel(tc, x, h0, gh0, w_words, w_scales, b_ih0, out)
         idle_work = keep.tile([P, P], F32)
         bias_rows = keep.tile([P, P], BF16)
         warm = keep.tile([P, 1], F32)
-        planes = keep.tile([P, PASSES, GATES * L], U8, align_bytes=64)
+        planes_r = keep.tile([P, PASSES, L], U8, align_bytes=64)
+        planes_zn = keep.tile([P, PASSES, 2 * L], U8, align_bytes=64)
         identity = keep.tile([P, P], F32)
         identity_bf = keep.tile([P, P], BF16)
         gh_sb = {}
@@ -48,19 +48,23 @@ def tile_grucellstack_pa_s_kernel(tc, x, h0, gh0, w_words, w_scales, b_ih0, out)
         nc.vector.memset(idle_work[:], 0.0)
         nc.vector.memset(warm[:], 0.0)
         nc.vector.memset(bias_rows[:], 0.0)
+        nc.gpsimd.dma_start(
+            out=bias_rows[0 : GATES * CHUNKS, :], in_=b_ih0.rearrange("(c p) -> c p", p=P)
+        )
         make_identity(nc, identity[:])
-        nc.gpsimd.dma_start(out=gh_sb[GATE_Z][:], in_=gh0[:, L * GATE_Z : L * (GATE_Z + 1)])
 
         x_sb = keep.tile([P, K], BF16)
         nc.sync.dma_start(out=x_sb[:], in_=x)
-        nc.sync.dma_start(out=gh_sb[GATE_R][:], in_=gh0[:, L * GATE_R : L * (GATE_R + 1)])
         nc.scalar.activation(out=warm[:], in_=warm[:], func=ACT.Sigmoid)
 
         scale_rows = w_scales.rearrange("g q n -> q g n")
-        for r in range(4):
-            nc.sync.dma_start(
-                out=planes[r:P:32, :, :].bitcast(I32), in_=scale_rows[r:16:4, :, :].bitcast(I32)
-            )
+
+        def load_scales(planes, first, width):
+            for r in range(4):
+                nc.sync.dma_start(
+                    out=planes[r:P:32, :, :].bitcast(I32),
+                    in_=scale_rows[r:16:4, :, first : first + width].bitcast(I32),
+                )
 
         word_rows = w_words.rearrange("g p n -> p g n")
         w_sb = {}
@@ -75,10 +79,11 @@ def tile_grucellstack_pa_s_kernel(tc, x, h0, gh0, w_words, w_scales, b_ih0, out)
         def load_gh(gate):
             nc.sync.dma_start(out=gh_sb[gate][:], in_=gh0[:, L * gate : L * (gate + 1)])
 
-        nc.sync.dma_start(
-            out=bias_rows[0 : GATES * CHUNKS, :], in_=b_ih0.rearrange("(c p) -> c p", p=P)
-        )
+        load_scales(planes_r, 0, L)
+        load_gh(GATE_R)
         load_words(GATE_R)
+        load_gh(GATE_Z)
+        load_scales(planes_zn, L, 2 * L)
         load_words(GATE_Z)
         load_gh(GATE_N)
         load_words(GATE_N)
@@ -90,15 +95,14 @@ def tile_grucellstack_pa_s_kernel(tc, x, h0, gh0, w_words, w_scales, b_ih0, out)
         x_codes = keep.tile([P, PASSES, P], U32, align_bytes=64)
         x_planes = keep.tile([P, PASSES, P], U8, align_bytes=64)
 
-        idle_out = psum.tile([P, P], F32, tag="z1")
-        for width in IDLE_WIDTHS:
-            nc.tensor.matmul(
-                out=idle_out[:, 0:width],
-                lhsT=idle_work[:],
-                rhs=idle_work[:, 0:width],
-                start=True,
-                stop=True,
-            )
+        def idle_matmuls(count, tag):
+            idle_out = psum.tile([P, P], F32, tag=tag)
+            for i in range(count):
+                nc.tensor.matmul(
+                    out=idle_out[:], lhsT=idle_work[:], rhs=idle_work[:], start=True, stop=True
+                )
+
+        idle_matmuls(3, "z1")
         x_words = x_sb[:].bitcast(F32)
         x_t = {}
         for g in range(PASSES):
@@ -136,6 +140,7 @@ def tile_grucellstack_pa_s_kernel(tc, x, h0, gh0, w_words, w_scales, b_ih0, out)
         gi = {}
 
         def multiply(gate, tags):
+            planes, first_col = (planes_r, 0) if gate == GATE_R else (planes_zn, L)
             for (first, count), tag in zip(PIECES, tags):
                 piece = psum.tile([P, count, P], F32, name="gi%d_%d" % (gate, first), tag=tag)
                 gi[(gate, first)] = piece
@@ -144,7 +149,7 @@ def tile_grucellstack_pa_s_kernel(tc, x, h0, gh0, w_words, w_scales, b_ih0, out)
                         nc.tensor.matmul_mx(
                             out=piece[:, c - first, :],
                             lhsT=w_sb[gate][:, g, 2 * P * c : 2 * P * (c + 1)].bitcast(FP4X4),
-                            lhsT_scale=planes[:, g, gate * L + P * c : gate * L + P * (c + 1)],
+                            lhsT_scale=planes[:, g, first_col + P * c : first_col + P * (c + 1)],
                             rhs=x_codes[:, g, :].bitcast(FP8X4),
                             rhs_scale=x_planes[:, g, :],
                             start=(g == 0),
@@ -161,12 +166,14 @@ def tile_grucellstack_pa_s_kernel(tc, x, h0, gh0, w_words, w_scales, b_ih0, out)
                         lhsT=x_codes[:, g, :].bitcast(FP8X4),
                         lhsT_scale=x_planes[:, g, :],
                         rhs=w_sb[GATE_Z][:, g, 2 * first : 2 * (first + width)].bitcast(FP4X4),
-                        rhs_scale=planes[:, g, L + first : L + first + width],
+                        rhs_scale=planes_zn[:, g, first : first + width],
                         start=(g == 0),
                         stop=(g == PASSES - 1),
                     )
 
         turn_gh(GATE_R, "z0")
+
+        idle_matmuls(2, "r0")
 
         bias_z = {}
         for (first, width), tag in zip(Z_PIECES, ("n0", "n1")):

@@ -38,23 +38,22 @@ def tile_grucellstack_pa_s_kernel(tc, x, h0, gh0, w_words, w_scales, b_ih0, out)
         idle_work = keep.tile([P, P], F32)
         bias_rows = keep.tile([P, P], BF16)
         warm = keep.tile([P, 1], F32)
-        planes_r = keep.tile([P, PASSES, L], U8, align_bytes=64)
-        planes_zn = keep.tile([P, PASSES, 2 * L], U8, align_bytes=64)
+        planes = keep.tile([P, PASSES, GATES * L], U8, align_bytes=64)
         identity = keep.tile([P, P], F32)
         identity_bf = keep.tile([P, P], BF16)
         gh_sb = {}
         for gate in range(GATES):
             gh_sb[gate] = keep.tile([P, L], BF16, name="gh_sb%d" % gate)
+        nc.vector.memset(bias_rows[:], 0.0)
         nc.vector.memset(idle_work[:], 0.0)
         nc.vector.memset(warm[:], 0.0)
-        nc.vector.memset(bias_rows[:], 0.0)
-        nc.gpsimd.dma_start(
-            out=bias_rows[0 : GATES * CHUNKS, :], in_=b_ih0.rearrange("(c p) -> c p", p=P)
-        )
         make_identity(nc, identity[:])
 
         x_sb = keep.tile([P, K], BF16)
         nc.sync.dma_start(out=x_sb[:], in_=x)
+        nc.scalar.dma_start(
+            out=bias_rows[0 : GATES * CHUNKS, :], in_=b_ih0.rearrange("(c p) -> c p", p=P)
+        )
         nc.scalar.activation(out=warm[:], in_=warm[:], func=ACT.Sigmoid)
 
         scale_rows = w_scales.rearrange("g q n -> q g n")
@@ -79,11 +78,10 @@ def tile_grucellstack_pa_s_kernel(tc, x, h0, gh0, w_words, w_scales, b_ih0, out)
         def load_gh(gate):
             nc.sync.dma_start(out=gh_sb[gate][:], in_=gh0[:, L * gate : L * (gate + 1)])
 
-        load_scales(planes_r, 0, L)
         load_gh(GATE_R)
+        load_scales(planes, 0, GATES * L)
         load_words(GATE_R)
         load_gh(GATE_Z)
-        load_scales(planes_zn, L, 2 * L)
         load_words(GATE_Z)
         load_gh(GATE_N)
         load_words(GATE_N)
@@ -112,9 +110,6 @@ def tile_grucellstack_pa_s_kernel(tc, x, h0, gh0, w_words, w_scales, b_ih0, out)
                     x_t[g][:, u, :], x_words[:, 256 * g + u : 256 * (g + 1) : 2], identity[:]
                 )
         nc.vector.tensor_copy(out=identity_bf[:], in_=identity[:])
-        bias_t = psum.tile([P, P], BF16, tag="z1")
-        nc.tensor.transpose(bias_t[:], bias_rows[:], identity_bf[:])
-        nc.vector.tensor_copy(out=bias_cols[:], in_=bias_t[:, 0 : GATES * CHUNKS])
         for g in range(PASSES):
             pairs = grouped[:, g].rearrange("p b t -> p (b t)").bitcast(F32)
             nc.scalar.copy(
@@ -140,7 +135,6 @@ def tile_grucellstack_pa_s_kernel(tc, x, h0, gh0, w_words, w_scales, b_ih0, out)
         gi = {}
 
         def multiply(gate, tags):
-            planes, first_col = (planes_r, 0) if gate == GATE_R else (planes_zn, L)
             for (first, count), tag in zip(PIECES, tags):
                 piece = psum.tile([P, count, P], F32, name="gi%d_%d" % (gate, first), tag=tag)
                 gi[(gate, first)] = piece
@@ -149,7 +143,7 @@ def tile_grucellstack_pa_s_kernel(tc, x, h0, gh0, w_words, w_scales, b_ih0, out)
                         nc.tensor.matmul_mx(
                             out=piece[:, c - first, :],
                             lhsT=w_sb[gate][:, g, 2 * P * c : 2 * P * (c + 1)].bitcast(FP4X4),
-                            lhsT_scale=planes[:, g, first_col + P * c : first_col + P * (c + 1)],
+                            lhsT_scale=planes[:, g, gate * L + P * c : gate * L + P * (c + 1)],
                             rhs=x_codes[:, g, :].bitcast(FP8X4),
                             rhs_scale=x_planes[:, g, :],
                             start=(g == 0),
@@ -166,7 +160,7 @@ def tile_grucellstack_pa_s_kernel(tc, x, h0, gh0, w_words, w_scales, b_ih0, out)
                         lhsT=x_codes[:, g, :].bitcast(FP8X4),
                         lhsT_scale=x_planes[:, g, :],
                         rhs=w_sb[GATE_Z][:, g, 2 * first : 2 * (first + width)].bitcast(FP4X4),
-                        rhs_scale=planes_zn[:, g, first : first + width],
+                        rhs_scale=planes[:, g, L + first : L + first + width],
                         start=(g == 0),
                         stop=(g == PASSES - 1),
                     )
@@ -174,6 +168,15 @@ def tile_grucellstack_pa_s_kernel(tc, x, h0, gh0, w_words, w_scales, b_ih0, out)
         turn_gh(GATE_R, "z0")
 
         idle_matmuls(2, "r0")
+        bias_t = psum.tile([P, P], BF16, tag="z1")
+        nc.tensor.transpose(bias_t[:], bias_rows[:], identity_bf[:])
+
+        gh_r_t = keep.tile([P, CHUNKS, P], BF16)
+        ghb_z = keep.tile([P, L], F32)
+
+        nc.vector.tensor_copy(out=gh_r_t[:], in_=gh_t[GATE_R][:])
+        nc.vector.tensor_copy(out=bias_cols[:], in_=bias_t[:, 0 : GATES * CHUNKS])
+        multiply(GATE_R, ("r0", "r1"))
 
         bias_z = {}
         for (first, width), tag in zip(Z_PIECES, ("n0", "n1")):
@@ -186,14 +189,6 @@ def tile_grucellstack_pa_s_kernel(tc, x, h0, gh0, w_words, w_scales, b_ih0, out)
                     identity[:],
                 )
 
-        gh_r_t = keep.tile([P, CHUNKS, P], BF16)
-        ghb_z = keep.tile([P, L], F32)
-
-        nc.vector.tensor_copy(out=gh_r_t[:], in_=gh_t[GATE_R][:])
-        for first, width in Z_PIECES:
-            cols = slice(first, first + width)
-            nc.vector.tensor_add(out=ghb_z[:, cols], in0=bias_z[first][:], in1=gh_sb[GATE_Z][:, cols])
-        multiply(GATE_R, ("r0", "r1"))
         multiply_z()
         turn_gh(GATE_N, "t0")
         multiply(GATE_N, ("n0", "n1"))
@@ -281,6 +276,9 @@ def tile_grucellstack_pa_s_kernel(tc, x, h0, gh0, w_words, w_scales, b_ih0, out)
         act(gate_r, pre_r, GATE_R, ACT.Sigmoid, A)
         add_gi(pre_r, GATE_R, B, gh_r_t)
         act(gate_r, pre_r, GATE_R, ACT.Sigmoid, B)
+        for first, width in Z_PIECES:
+            cols = slice(first, first + width)
+            nc.vector.tensor_add(out=ghb_z[:, cols], in0=bias_z[first][:], in1=gh_sb[GATE_Z][:, cols])
         gate_z_of(A)
         gate_z_of(B)
         times_gh_n(A)

@@ -22,7 +22,7 @@ GATE_R, GATE_Z, GATE_N = 0, 1, 2
 GATES = 3
 CHUNKS = L // P
 
-PIECES = ((0, 3), (3, 2))
+PIECES = ((0, 2), (2, 2), (4, 1))
 Z_PIECES = ((0, 512), (512, 128))
 
 FLOPS = 2 * P * K * GATES * L
@@ -51,10 +51,6 @@ def tile_grucellstack_pa_s_kernel(tc, x, h0, gh0, w_words, w_scales, b_ih0, out)
 
         x_sb = keep.tile([P, K], BF16)
         nc.sync.dma_start(out=x_sb[:], in_=x)
-        nc.scalar.dma_start(
-            out=bias_rows[0 : GATES * CHUNKS, :], in_=b_ih0.rearrange("(c p) -> c p", p=P)
-        )
-        nc.scalar.activation(out=warm[:], in_=warm[:], func=ACT.Sigmoid)
 
         scale_rows = w_scales.rearrange("g q n -> q g n")
 
@@ -81,6 +77,10 @@ def tile_grucellstack_pa_s_kernel(tc, x, h0, gh0, w_words, w_scales, b_ih0, out)
         load_gh(GATE_R)
         load_scales(planes, 0, GATES * L)
         load_words(GATE_R)
+        nc.scalar.dma_start(
+            out=bias_rows[0 : GATES * CHUNKS, :], in_=b_ih0.rearrange("(c p) -> c p", p=P)
+        )
+        nc.scalar.activation(out=warm[:], in_=warm[:], func=ACT.Sigmoid)
         load_gh(GATE_Z)
         load_words(GATE_Z)
         load_gh(GATE_N)
@@ -100,11 +100,11 @@ def tile_grucellstack_pa_s_kernel(tc, x, h0, gh0, w_words, w_scales, b_ih0, out)
                     out=idle_out[:], lhsT=idle_work[:], rhs=idle_work[:], start=True, stop=True
                 )
 
-        idle_matmuls(3, "z1")
+        idle_matmuls(3, "k4")
         x_words = x_sb[:].bitcast(F32)
         x_t = {}
         for g in range(PASSES):
-            x_t[g] = psum.tile([P, 2, P], F32, name="x_t%d" % g, tag="t%d" % g)
+            x_t[g] = psum.tile([P, 2, P], F32, name="x_t%d" % g, tag="k%d" % (5 + g))
             for u in range(2):
                 nc.tensor.transpose(
                     x_t[g][:, u, :], x_words[:, 256 * g + u : 256 * (g + 1) : 2], identity[:]
@@ -151,7 +151,7 @@ def tile_grucellstack_pa_s_kernel(tc, x, h0, gh0, w_words, w_scales, b_ih0, out)
                         )
 
         def multiply_z():
-            for (first, width), tag in zip(Z_PIECES, ("z0", "z1")):
+            for (first, width), tag in zip(Z_PIECES, ("k3", "k4")):
                 piece = psum.tile([P, width], F32, name="gi_z%d" % first, tag=tag)
                 gi[(GATE_Z, first)] = piece
                 for g in range(PASSES):
@@ -165,21 +165,22 @@ def tile_grucellstack_pa_s_kernel(tc, x, h0, gh0, w_words, w_scales, b_ih0, out)
                         stop=(g == PASSES - 1),
                     )
 
-        turn_gh(GATE_R, "z0")
-
-        idle_matmuls(2, "r0")
-        bias_t = psum.tile([P, P], BF16, tag="z1")
+        idle_matmuls(1, "k4")
+        turn_gh(GATE_R, "k3")
+        idle_matmuls(1, "k4")
+        bias_t = psum.tile([P, P], BF16, tag="k7")
         nc.tensor.transpose(bias_t[:], bias_rows[:], identity_bf[:])
+        idle_matmuls(1, "k4")
 
         gh_r_t = keep.tile([P, CHUNKS, P], BF16)
         ghb_z = keep.tile([P, L], F32)
 
         nc.vector.tensor_copy(out=gh_r_t[:], in_=gh_t[GATE_R][:])
         nc.vector.tensor_copy(out=bias_cols[:], in_=bias_t[:, 0 : GATES * CHUNKS])
-        multiply(GATE_R, ("r0", "r1"))
+        multiply(GATE_R, ("k0", "k1", "k2"))
 
         bias_z = {}
-        for (first, width), tag in zip(Z_PIECES, ("n0", "n1")):
+        for (first, width), tag in zip(Z_PIECES, ("k5", "k6")):
             bias_z[first] = psum.tile([P, width], F32, name="bias_z%d" % first, tag=tag)
             for c in range(width // P):
                 col = GATE_Z * CHUNKS + first // P + c
@@ -190,8 +191,9 @@ def tile_grucellstack_pa_s_kernel(tc, x, h0, gh0, w_words, w_scales, b_ih0, out)
                 )
 
         multiply_z()
-        turn_gh(GATE_N, "t0")
-        multiply(GATE_N, ("n0", "n1"))
+        turn_gh(GATE_N, "k7")
+        multiply(GATE_N, ("k0", "k1", "k2"))
+        idle_matmuls(2, "k6")
 
         pre_r = keep.tile([P, CHUNKS, P], F32)
         pre_n = keep.tile([P, CHUNKS, P], F32)
@@ -204,7 +206,7 @@ def tile_grucellstack_pa_s_kernel(tc, x, h0, gh0, w_words, w_scales, b_ih0, out)
         z_h = keep.tile([P, L], F32)
         blend = keep.tile([P, L], F32)
 
-        A, B = 0, 1
+        A, B, C = range(len(PIECES))
 
         def chunks_of(piece):
             first, count = PIECES[piece]
@@ -272,26 +274,28 @@ def tile_grucellstack_pa_s_kernel(tc, x, h0, gh0, w_words, w_scales, b_ih0, out)
             nc.vector.tensor_sub(out=blend[:, cols], in0=z_h[:, cols], in1=part_n[:, cols])
             nc.sync.dma_start(out=out[:, cols], in_=blend[:, cols])
 
-        add_gi(pre_r, GATE_R, A, gh_r_t)
-        act(gate_r, pre_r, GATE_R, ACT.Sigmoid, A)
-        add_gi(pre_r, GATE_R, B, gh_r_t)
-        act(gate_r, pre_r, GATE_R, ACT.Sigmoid, B)
+        for piece in (A, B, C):
+            add_gi(pre_r, GATE_R, piece, gh_r_t)
+            act(gate_r, pre_r, GATE_R, ACT.Sigmoid, piece)
         for first, width in Z_PIECES:
             cols = slice(first, first + width)
             nc.vector.tensor_add(out=ghb_z[:, cols], in0=bias_z[first][:], in1=gh_sb[GATE_Z][:, cols])
-        gate_z_of(A)
-        gate_z_of(B)
+        gate_z_of(0)
         times_gh_n(A)
+        gate_z_of(1)
         times_gh_n(B)
-        add_gi(pre_n, GATE_N, A, r_gh)
-        act(gate_n, pre_n, GATE_N, ACT.Tanh, A)
-        add_gi(pre_n, GATE_N, B, r_gh)
-        act(gate_n, pre_n, GATE_N, ACT.Tanh, B)
-        times_h(A)
-        times_h(B)
-        turn_back(A, "r0")
-        turn_back(B, "r1")
+        times_gh_n(C)
+        for piece in (A, B, C):
+            add_gi(pre_n, GATE_N, piece, r_gh)
+            act(gate_n, pre_n, GATE_N, ACT.Tanh, piece)
+        for piece in (A, B, C):
+            times_h(piece)
+        turn_back(A, "k3")
+        turn_back(B, "k4")
+        turn_back(C, "k5")
         minus_part_n(A)
         minus_part_n(B)
         finish(A)
+        minus_part_n(C)
         finish(B)
+        finish(C)

@@ -51,6 +51,7 @@ def tile_grucellstack_pa_s_kernel(tc, x, h0, gh0, w_words, w_scales, b_ih0, out)
 
         x_sb = keep.tile([P, K], BF16)
         nc.sync.dma_start(out=x_sb[:], in_=x)
+        nc.scalar.activation(out=warm[:], in_=warm[:], func=ACT.Sigmoid)
 
         scale_rows = w_scales.rearrange("g q n -> q g n")
 
@@ -77,10 +78,9 @@ def tile_grucellstack_pa_s_kernel(tc, x, h0, gh0, w_words, w_scales, b_ih0, out)
         load_gh(GATE_R)
         load_scales(planes, 0, GATES * L)
         load_words(GATE_R)
-        nc.scalar.dma_start(
+        nc.sync.dma_start(
             out=bias_rows[0 : GATES * CHUNKS, :], in_=b_ih0.rearrange("(c p) -> c p", p=P)
         )
-        nc.scalar.activation(out=warm[:], in_=warm[:], func=ACT.Sigmoid)
         load_gh(GATE_Z)
         load_words(GATE_Z)
         load_gh(GATE_N)

@@ -22,7 +22,7 @@ GATE_R, GATE_Z, GATE_N = 0, 1, 2
 GATES = 3
 CHUNKS = L // P
 
-PIECES = ((0, 2), (2, 2), (4, 1))
+PIECES = ((0, 1), (1, 2), (3, 2))
 Z_PIECES = ((0, 512), (512, 128))
 
 FLOPS = 2 * P * K * GATES * L
@@ -36,17 +36,18 @@ def tile_grucellstack_pa_s_kernel(tc, x, h0, gh0, w_words, w_scales, b_ih0, out)
         psum = ctx.enter_context(tc.psum_pool(name="psum", bufs=1))
 
         idle_work = keep.tile([P, P], F32)
-        bias_rows = keep.tile([P, P], BF16)
+        bias_row = keep.tile([P, GATES * L], BF16)
         warm = keep.tile([P, 1], F32)
-        planes = keep.tile([P, PASSES, GATES * L], U8, align_bytes=64)
+        planes_r = keep.tile([P, PASSES, L], U8, align_bytes=64)
+        planes_zn = keep.tile([P, PASSES, 2 * L], U8, align_bytes=64)
         identity = keep.tile([P, P], F32)
         identity_bf = keep.tile([P, P], BF16)
-        gh_sb = {}
-        for gate in range(GATES):
-            gh_sb[gate] = keep.tile([P, L], BF16, name="gh_sb%d" % gate)
-        nc.vector.memset(bias_rows[:], 0.0)
+        gh_rz = keep.tile([P, 2 * L], BF16)
+        gh_n = keep.tile([P, L], BF16)
         nc.vector.memset(idle_work[:], 0.0)
         nc.vector.memset(warm[:], 0.0)
+        nc.gpsimd.memset(bias_row[:, 0 : GATES * L // 2].bitcast(I32), 0)
+        nc.vector.memset(bias_row[:, GATES * L // 2 :].bitcast(I32), 0)
         make_identity(nc, identity[:])
 
         x_sb = keep.tile([P, K], BF16)
@@ -72,23 +73,18 @@ def tile_grucellstack_pa_s_kernel(tc, x, h0, gh0, w_words, w_scales, b_ih0, out)
                 in_=word_rows[:, :, 2 * L * gate : 2 * L * (gate + 1)].bitcast(I32),
             )
 
-        def load_gh(gate):
-            nc.sync.dma_start(out=gh_sb[gate][:], in_=gh0[:, L * gate : L * (gate + 1)])
-
-        load_gh(GATE_R)
-        load_scales(planes, 0, GATES * L)
+        nc.sync.dma_start(out=gh_rz[:], in_=gh0[:, 0 : 2 * L])
+        load_scales(planes_r, 0, L)
+        nc.sync.dma_start(out=bias_row[0:1, :], in_=b_ih0.rearrange("(o n) -> o n", o=1))
         load_words(GATE_R)
-        nc.sync.dma_start(
-            out=bias_rows[0 : GATES * CHUNKS, :], in_=b_ih0.rearrange("(c p) -> c p", p=P)
-        )
-        load_gh(GATE_Z)
+        load_scales(planes_zn, L, 2 * L)
         load_words(GATE_Z)
-        load_gh(GATE_N)
+        nc.sync.dma_start(out=gh_n[:], in_=gh0[:, 2 * L : 3 * L])
         load_words(GATE_N)
         h_sb = keep.tile([P, L], BF16)
         nc.sync.dma_start(out=h_sb[:], in_=h0)
 
-        bias_cols = keep.tile([P, GATES * CHUNKS], F32)
+        bias_cols = keep.tile([P, 2 * CHUNKS], F32)
         grouped = keep.tile([P, PASSES, P, PACK], BF16, align_bytes=64)
         x_codes = keep.tile([P, PASSES, P], U32, align_bytes=64)
         x_planes = keep.tile([P, PASSES, P], U8, align_bytes=64)
@@ -125,16 +121,17 @@ def tile_grucellstack_pa_s_kernel(tc, x, h0, gh0, w_words, w_scales, b_ih0, out)
 
         gh_t = {}
 
-        def turn_gh(gate, tag):
+        def turn_gh(gate, source, tag):
             gh_t[gate] = psum.tile([P, CHUNKS, P], BF16, name="gh_t%d" % gate, tag=tag)
             for c in range(CHUNKS):
                 nc.tensor.transpose(
-                    gh_t[gate][:, c, :], gh_sb[gate][:, P * c : P * (c + 1)], identity_bf[:]
+                    gh_t[gate][:, c, :], source[:, P * c : P * (c + 1)], identity_bf[:]
                 )
 
         gi = {}
 
         def multiply(gate, tags):
+            planes, first_col = (planes_r, 0) if gate == GATE_R else (planes_zn, L)
             for (first, count), tag in zip(PIECES, tags):
                 piece = psum.tile([P, count, P], F32, name="gi%d_%d" % (gate, first), tag=tag)
                 gi[(gate, first)] = piece
@@ -143,7 +140,7 @@ def tile_grucellstack_pa_s_kernel(tc, x, h0, gh0, w_words, w_scales, b_ih0, out)
                         nc.tensor.matmul_mx(
                             out=piece[:, c - first, :],
                             lhsT=w_sb[gate][:, g, 2 * P * c : 2 * P * (c + 1)].bitcast(FP4X4),
-                            lhsT_scale=planes[:, g, gate * L + P * c : gate * L + P * (c + 1)],
+                            lhsT_scale=planes[:, g, first_col + P * c : first_col + P * (c + 1)],
                             rhs=x_codes[:, g, :].bitcast(FP8X4),
                             rhs_scale=x_planes[:, g, :],
                             start=(g == 0),
@@ -160,40 +157,48 @@ def tile_grucellstack_pa_s_kernel(tc, x, h0, gh0, w_words, w_scales, b_ih0, out)
                         lhsT=x_codes[:, g, :].bitcast(FP8X4),
                         lhsT_scale=x_planes[:, g, :],
                         rhs=w_sb[GATE_Z][:, g, 2 * first : 2 * (first + width)].bitcast(FP4X4),
-                        rhs_scale=planes[:, g, L + first : L + first + width],
+                        rhs_scale=planes_zn[:, g, first : first + width],
                         start=(g == 0),
                         stop=(g == PASSES - 1),
                     )
 
-        idle_matmuls(1, "k4")
-        turn_gh(GATE_R, "k3")
-        idle_matmuls(1, "k4")
-        bias_t = psum.tile([P, P], BF16, tag="k7")
-        nc.tensor.transpose(bias_t[:], bias_rows[:], identity_bf[:])
-        idle_matmuls(1, "k4")
-
+        turn_gh(GATE_R, gh_rz[:, 0:L], "k3")
         gh_r_t = keep.tile([P, CHUNKS, P], BF16)
-        ghb_z = keep.tile([P, L], F32)
-
-        nc.vector.tensor_copy(out=gh_r_t[:], in_=gh_t[GATE_R][:])
-        nc.vector.tensor_copy(out=bias_cols[:], in_=bias_t[:, 0 : GATES * CHUNKS])
-        multiply(GATE_R, ("k0", "k1", "k2"))
+        nc.scalar.copy(out=gh_r_t[:], in_=gh_t[GATE_R][:])
 
         bias_z = {}
         for (first, width), tag in zip(Z_PIECES, ("k5", "k6")):
             bias_z[first] = psum.tile([P, width], F32, name="bias_z%d" % first, tag=tag)
-            for c in range(width // P):
-                col = GATE_Z * CHUNKS + first // P + c
-                nc.tensor.transpose(
-                    bias_z[first][:, P * c : P * (c + 1)],
-                    bias_cols[:, col : col + 1].to_broadcast([P, P]),
-                    identity[:],
-                )
+            nc.tensor.matmul(
+                out=bias_z[first][:],
+                lhsT=identity_bf[:, 0:1].to_broadcast([P, P]),
+                rhs=bias_row[:, L + first : L + first + width],
+                start=True,
+                stop=True,
+            )
+        bias_t = psum.tile([P, 2 * CHUNKS], F32, tag="k7")
+        for i in range(2 * CHUNKS):
+            first = P * i if i < CHUNKS else 2 * L + P * (i - CHUNKS)
+            nc.tensor.matmul(
+                out=bias_t[:, i : i + 1],
+                lhsT=bias_row[:, first : first + P],
+                rhs=identity_bf[:, 0:1],
+                start=True,
+                stop=True,
+            )
 
+        ghb_z = keep.tile([P, L], F32)
+        for first, width in Z_PIECES:
+            nc.vector.tensor_add(
+                out=ghb_z[:, first : first + width],
+                in0=bias_z[first][:],
+                in1=gh_rz[:, L + first : L + first + width],
+            )
+        nc.vector.tensor_copy(out=bias_cols[:], in_=bias_t[:])
+        multiply(GATE_R, ("k0", "k1", "k2"))
         multiply_z()
-        turn_gh(GATE_N, "k7")
+        turn_gh(GATE_N, gh_n, "k7")
         multiply(GATE_N, ("k0", "k1", "k2"))
-        idle_matmuls(2, "k6")
 
         pre_r = keep.tile([P, CHUNKS, P], F32)
         pre_n = keep.tile([P, CHUNKS, P], F32)
@@ -225,12 +230,13 @@ def tile_grucellstack_pa_s_kernel(tc, x, h0, gh0, w_words, w_scales, b_ih0, out)
 
         def act(out_tile, in_tile, gate, func, piece):
             first, count = PIECES[piece]
+            column = 0 if gate == GATE_R else CHUNKS
             for c in range(first, first + count):
                 nc.scalar.activation(
                     out=out_tile[:, c, :],
                     in_=in_tile[:, c, :],
                     func=func,
-                    bias=bias_cols[:, gate * CHUNKS + c : gate * CHUNKS + c + 1],
+                    bias=bias_cols[:, column + c : column + c + 1],
                 )
 
         def gate_z_of(piece):
@@ -254,9 +260,9 @@ def tile_grucellstack_pa_s_kernel(tc, x, h0, gh0, w_words, w_scales, b_ih0, out)
             for c in range(first, first + count):
                 nc.tensor.transpose(n_back[piece][:, c - first, :], gate_n[:, c, :], identity[:])
 
-        def times_h(piece):
+        def times_h(engine, piece):
             cols = cols_of(piece)
-            nc.vector.tensor_mul(out=z_h[:, cols], in0=gate_z[:, cols], in1=h_sb[:, cols])
+            engine.tensor_mul(out=z_h[:, cols], in0=gate_z[:, cols], in1=h_sb[:, cols])
 
         def minus_part_n(piece):
             cols = cols_of(piece)
@@ -277,19 +283,17 @@ def tile_grucellstack_pa_s_kernel(tc, x, h0, gh0, w_words, w_scales, b_ih0, out)
         for piece in (A, B, C):
             add_gi(pre_r, GATE_R, piece, gh_r_t)
             act(gate_r, pre_r, GATE_R, ACT.Sigmoid, piece)
-        for first, width in Z_PIECES:
-            cols = slice(first, first + width)
-            nc.vector.tensor_add(out=ghb_z[:, cols], in0=bias_z[first][:], in1=gh_sb[GATE_Z][:, cols])
         gate_z_of(0)
         times_gh_n(A)
-        gate_z_of(1)
         times_gh_n(B)
+        gate_z_of(1)
         times_gh_n(C)
+        times_h(nc.gpsimd, A)
+        times_h(nc.gpsimd, B)
         for piece in (A, B, C):
             add_gi(pre_n, GATE_N, piece, r_gh)
             act(gate_n, pre_n, GATE_N, ACT.Tanh, piece)
-        for piece in (A, B, C):
-            times_h(piece)
+        times_h(nc.vector, C)
         turn_back(A, "k3")
         turn_back(B, "k4")
         turn_back(C, "k5")

@@ -84,7 +84,7 @@ def tile_grucellstack_pa_s_kernel(tc, x, h0, gh0, w_words, w_scales, b_ih0, out)
         h_sb = keep.tile([P, L], BF16)
         nc.sync.dma_start(out=h_sb[:], in_=h0)
 
-        bias_cols = keep.tile([P, 2 * CHUNKS], F32)
+        bias_cols = {}
         grouped = keep.tile([P, PASSES, P, PACK], BF16, align_bytes=64)
         x_codes = keep.tile([P, PASSES, P], U32, align_bytes=64)
         x_planes = keep.tile([P, PASSES, P], U8, align_bytes=64)
@@ -176,16 +176,19 @@ def tile_grucellstack_pa_s_kernel(tc, x, h0, gh0, w_words, w_scales, b_ih0, out)
                 start=True,
                 stop=True,
             )
-        bias_t = psum.tile([P, 2 * CHUNKS], F32, tag="k7")
-        for i in range(2 * CHUNKS):
-            first = P * i if i < CHUNKS else 2 * L + P * (i - CHUNKS)
-            nc.tensor.matmul(
-                out=bias_t[:, i : i + 1],
-                lhsT=bias_row[:, first : first + P],
-                rhs=identity_bf[:, 0:1],
-                start=True,
-                stop=True,
-            )
+        def turn_bias(gate, tag):
+            bias_t = psum.tile([P, CHUNKS], F32, name="bias_t%d" % gate, tag=tag)
+            for c in range(CHUNKS):
+                first = gate * L + P * c
+                nc.tensor.matmul(
+                    out=bias_t[:, c : c + 1],
+                    lhsT=bias_row[:, first : first + P],
+                    rhs=identity_bf[:, 0:1],
+                    start=True,
+                    stop=True,
+                )
+            bias_cols[gate] = keep.tile([P, CHUNKS], F32, name="bias_cols%d" % gate)
+            nc.vector.tensor_copy(out=bias_cols[gate][:], in_=bias_t[:])
 
         ghb_z = keep.tile([P, L], F32)
         for first, width in Z_PIECES:
@@ -194,7 +197,8 @@ def tile_grucellstack_pa_s_kernel(tc, x, h0, gh0, w_words, w_scales, b_ih0, out)
                 in0=bias_z[first][:],
                 in1=gh_rz[:, L + first : L + first + width],
             )
-        nc.vector.tensor_copy(out=bias_cols[:], in_=bias_t[:])
+        turn_bias(GATE_R, "k7")
+        idle_matmuls(1, "k4")
         multiply(GATE_R, ("k0", "k1", "k2"))
         multiply_z()
         turn_gh(GATE_N, gh_n, "k7")
@@ -230,13 +234,12 @@ def tile_grucellstack_pa_s_kernel(tc, x, h0, gh0, w_words, w_scales, b_ih0, out)
 
         def act(out_tile, in_tile, gate, func, piece):
             first, count = PIECES[piece]
-            column = 0 if gate == GATE_R else CHUNKS
             for c in range(first, first + count):
                 nc.scalar.activation(
                     out=out_tile[:, c, :],
                     in_=in_tile[:, c, :],
                     func=func,
-                    bias=bias_cols[:, column + c : column + c + 1],
+                    bias=bias_cols[gate][:, c : c + 1],
                 )
 
         def gate_z_of(piece):
@@ -288,6 +291,7 @@ def tile_grucellstack_pa_s_kernel(tc, x, h0, gh0, w_words, w_scales, b_ih0, out)
         times_gh_n(B)
         gate_z_of(1)
         times_gh_n(C)
+        turn_bias(GATE_N, "k6")
         times_h(nc.gpsimd, A)
         times_h(nc.gpsimd, B)
         for piece in (A, B, C):

@@ -38,8 +38,7 @@ def tile_grucellstack_pa_s_kernel(tc, x, h0, gh0, w_words, w_scales, b_ih0, out)
         idle_work = keep.tile([P, P], F32)
         bias_row = keep.tile([P, GATES * L], BF16)
         warm = keep.tile([P, 1], F32)
-        planes_r = keep.tile([P, PASSES, L], U8, align_bytes=64)
-        planes_zn = keep.tile([P, PASSES, 2 * L], U8, align_bytes=64)
+        planes = keep.tile([P, PASSES, GATES * L], U8, align_bytes=64)
         identity = keep.tile([P, P], F32)
         identity_bf = keep.tile([P, P], BF16)
         gh_rz = keep.tile([P, 2 * L], BF16)
@@ -74,10 +73,9 @@ def tile_grucellstack_pa_s_kernel(tc, x, h0, gh0, w_words, w_scales, b_ih0, out)
             )
 
         nc.sync.dma_start(out=gh_rz[:], in_=gh0[:, 0 : 2 * L])
-        load_scales(planes_r, 0, L)
+        load_scales(planes, 0, GATES * L)
         nc.sync.dma_start(out=bias_row[0:1, :], in_=b_ih0.rearrange("(o n) -> o n", o=1))
         load_words(GATE_R)
-        load_scales(planes_zn, L, 2 * L)
         load_words(GATE_Z)
         nc.sync.dma_start(out=gh_n[:], in_=gh0[:, 2 * L : 3 * L])
         load_words(GATE_N)
@@ -131,7 +129,6 @@ def tile_grucellstack_pa_s_kernel(tc, x, h0, gh0, w_words, w_scales, b_ih0, out)
         gi = {}
 
         def multiply(gate, tags):
-            planes, first_col = (planes_r, 0) if gate == GATE_R else (planes_zn, L)
             for (first, count), tag in zip(PIECES, tags):
                 piece = psum.tile([P, count, P], F32, name="gi%d_%d" % (gate, first), tag=tag)
                 gi[(gate, first)] = piece
@@ -140,7 +137,7 @@ def tile_grucellstack_pa_s_kernel(tc, x, h0, gh0, w_words, w_scales, b_ih0, out)
                         nc.tensor.matmul_mx(
                             out=piece[:, c - first, :],
                             lhsT=w_sb[gate][:, g, 2 * P * c : 2 * P * (c + 1)].bitcast(FP4X4),
-                            lhsT_scale=planes[:, g, first_col + P * c : first_col + P * (c + 1)],
+                            lhsT_scale=planes[:, g, gate * L + P * c : gate * L + P * (c + 1)],
                             rhs=x_codes[:, g, :].bitcast(FP8X4),
                             rhs_scale=x_planes[:, g, :],
                             start=(g == 0),
@@ -157,11 +154,12 @@ def tile_grucellstack_pa_s_kernel(tc, x, h0, gh0, w_words, w_scales, b_ih0, out)
                         lhsT=x_codes[:, g, :].bitcast(FP8X4),
                         lhsT_scale=x_planes[:, g, :],
                         rhs=w_sb[GATE_Z][:, g, 2 * first : 2 * (first + width)].bitcast(FP4X4),
-                        rhs_scale=planes_zn[:, g, first : first + width],
+                        rhs_scale=planes[:, g, L + first : L + first + width],
                         start=(g == 0),
                         stop=(g == PASSES - 1),
                     )
 
+        idle_matmuls(1, "k4")
         turn_gh(GATE_R, gh_rz[:, 0:L], "k3")
         gh_r_t = keep.tile([P, CHUNKS, P], BF16)
         nc.scalar.copy(out=gh_r_t[:], in_=gh_t[GATE_R][:])
@@ -198,7 +196,6 @@ def tile_grucellstack_pa_s_kernel(tc, x, h0, gh0, w_words, w_scales, b_ih0, out)
                 in1=gh_rz[:, L + first : L + first + width],
             )
         turn_bias(GATE_R, "k7")
-        idle_matmuls(1, "k4")
         multiply(GATE_R, ("k0", "k1", "k2"))
         multiply_z()
         turn_gh(GATE_N, gh_n, "k7")

from contextlib import ExitStack

import concourse.mybir as mybir
from concourse.masks import make_identity

F32 = mybir.dt.float32
BF16 = mybir.dt.bfloat16
I32 = mybir.dt.int32
U32 = mybir.dt.uint32
U8 = mybir.dt.uint8
FP8X4 = mybir.dt.float8_e4m3fn_x4
FP4X4 = mybir.dt.float4_e2m1fn_x4
ACT = mybir.ActivationFunctionType
ALU = mybir.AluOpType

P = 128
PACK = 4
K = 1024
PASSES = K // (P * PACK)
L = 640
GATE_R, GATE_Z, GATE_N = 0, 1, 2
GATES = 3
CHUNKS = L // P

PIECES = ((0, 1), (1, 2), (3, 2))
Z_PIECES = ((0, 512), (512, 128))

FLOPS = 2 * P * K * GATES * L


def tile_grucellstack_pa_s_kernel(tc, x, h0, gh0, w_words, w_scales, b_ih0, out):
    nc = tc.nc
    with ExitStack() as ctx:
        ctx.enter_context(tc.manual_schedule())
        keep = ctx.enter_context(tc.tile_pool(name="keep", bufs=1))
        psum = ctx.enter_context(tc.psum_pool(name="psum", bufs=1))

        idle_work = keep.tile([P, P], F32)
        bias_row = keep.tile([P, GATES * L], BF16)
        warm = keep.tile([P, 1], F32)
        planes = keep.tile([P, PASSES, GATES * L], U8, align_bytes=64)
        identity = keep.tile([P, P], F32)
        identity_bf = keep.tile([P, P], BF16)
        gh_rz = keep.tile([P, 2 * L], BF16)
        gh_n = keep.tile([P, L], BF16)
        nc.vector.memset(idle_work[:], 0.0)
        nc.vector.memset(warm[:], 0.0)
        nc.gpsimd.memset(bias_row[:, 0 : GATES * L // 2].bitcast(I32), 0)
        nc.vector.memset(bias_row[:, GATES * L // 2 :].bitcast(I32), 0)
        make_identity(nc, identity[:])

        x_sb = keep.tile([P, K], BF16)
        nc.sync.dma_start(out=x_sb[:], in_=x)
        nc.scalar.activation(out=warm[:], in_=warm[:], func=ACT.Sigmoid)

        scale_rows = w_scales.rearrange("g q n -> q g n")

        def load_scales(planes, first, width):
            for r in range(4):
                nc.sync.dma_start(
                    out=planes[r:P:32, :, :].bitcast(I32),
                    in_=scale_rows[r:16:4, :, first : first + width].bitcast(I32),
                )

        word_rows = w_words.rearrange("g p n -> p g n")
        w_sb = {}

        def load_words(gate):
            w_sb[gate] = keep.tile([P, PASSES, 2 * L], U8, align_bytes=64, name="w_sb%d" % gate)
            nc.sync.dma_start(
                out=w_sb[gate][:].bitcast(I32),
                in_=word_rows[:, :, 2 * L * gate : 2 * L * (gate + 1)].bitcast(I32),
            )

        nc.sync.dma_start(out=gh_rz[:], in_=gh0[:, 0 : 2 * L])
        load_scales(planes, 0, GATES * L)
        nc.sync.dma_start(out=bias_row[0:1, :], in_=b_ih0.rearrange("(o n) -> o n", o=1))
        load_words(GATE_R)
        load_words(GATE_Z)
        nc.sync.dma_start(out=gh_n[:], in_=gh0[:, 2 * L : 3 * L])
        load_words(GATE_N)
        h_sb = keep.tile([P, L], BF16)
        nc.sync.dma_start(out=h_sb[:], in_=h0)

        bias_cols = {}
        grouped = keep.tile([P, PASSES, P, PACK], BF16, align_bytes=64)
        x_codes = keep.tile([P, PASSES, P], U32, align_bytes=64)
        x_planes = keep.tile([P, PASSES, P], U8, align_bytes=64)

        def idle_matmuls(count, tag):
            idle_out = psum.tile([P, P], F32, tag=tag)
            for i in range(count):
                nc.tensor.matmul(
                    out=idle_out[:], lhsT=idle_work[:], rhs=idle_work[:], start=True, stop=True
                )

        idle_matmuls(3, "k4")
        x_words = x_sb[:].bitcast(F32)
        x_t = {}
        for g in range(PASSES):
            x_t[g] = psum.tile([P, 2, P], F32, name="x_t%d" % g, tag="k%d" % (5 + g))
            for u in range(2):
                nc.tensor.transpose(
                    x_t[g][:, u, :], x_words[:, 256 * g + u : 256 * (g + 1) : 2], identity[:]
                )
        nc.vector.tensor_copy(out=identity_bf[:], in_=identity[:])
        for g in range(PASSES):
            pairs = grouped[:, g].rearrange("p b t -> p (b t)").bitcast(F32)
            nc.scalar.copy(
                out=pairs.rearrange("p (b u) -> p b u", u=2),
                in_=x_t[g][:].rearrange("p u b -> p b u"),
            )
        for g in range(PASSES):
            nc.vector.quantize_mx(
                out=x_codes[:, g, :].bitcast(FP8X4),
                scales=x_planes[:, g, :],
                in_=grouped[:, g].rearrange("p b t -> p (b t)"),
            )

        gh_t = {}

        def turn_gh(gate, source, tag):
            gh_t[gate] = psum.tile([P, CHUNKS, P], BF16, name="gh_t%d" % gate, tag=tag)
            for c in range(CHUNKS):
                nc.tensor.transpose(
                    gh_t[gate][:, c, :], source[:, P * c : P * (c + 1)], identity_bf[:]
                )

        gi = {}

        def multiply(gate, tags):
            for (first, count), tag in zip(PIECES, tags):
                piece = psum.tile([P, count, P], F32, name="gi%d_%d" % (gate, first), tag=tag)
                gi[(gate, first)] = piece
                for c in range(first, first + count):
                    for g in range(PASSES):
                        nc.tensor.matmul_mx(
                            out=piece[:, c - first, :],
                            lhsT=w_sb[gate][:, g, 2 * P * c : 2 * P * (c + 1)].bitcast(FP4X4),
                            lhsT_scale=planes[:, g, gate * L + P * c : gate * L + P * (c + 1)],
                            rhs=x_codes[:, g, :].bitcast(FP8X4),
                            rhs_scale=x_planes[:, g, :],
                            start=(g == 0),
                            stop=(g == PASSES - 1),
                        )

        def multiply_z():
            for (first, width), tag in zip(Z_PIECES, ("k3", "k4")):
                piece = psum.tile([P, width], F32, name="gi_z%d" % first, tag=tag)
                gi[(GATE_Z, first)] = piece
                for g in range(PASSES):
                    nc.tensor.matmul_mx(
                        out=piece[:],
                        lhsT=x_codes[:, g, :].bitcast(FP8X4),
                        lhsT_scale=x_planes[:, g, :],
                        rhs=w_sb[GATE_Z][:, g, 2 * first : 2 * (first + width)].bitcast(FP4X4),
                        rhs_scale=planes[:, g, L + first : L + first + width],
                        start=(g == 0),
                        stop=(g == PASSES - 1),
                    )

        idle_matmuls(1, "k4")
        turn_gh(GATE_R, gh_rz[:, 0:L], "k3")
        gh_r_t = keep.tile([P, CHUNKS, P], BF16)
        nc.scalar.copy(out=gh_r_t[:], in_=gh_t[GATE_R][:])

        bias_z = {}
        for (first, width), tag in zip(Z_PIECES, ("k5", "k6")):
            bias_z[first] = psum.tile([P, width], F32, name="bias_z%d" % first, tag=tag)
            nc.tensor.matmul(
                out=bias_z[first][:],
                lhsT=identity_bf[:, 0:1].to_broadcast([P, P]),
                rhs=bias_row[:, L + first : L + first + width],
                start=True,
                stop=True,
            )
        def turn_bias(gate, tag):
            bias_t = psum.tile([P, CHUNKS], F32, name="bias_t%d" % gate, tag=tag)
            for c in range(CHUNKS):
                first = gate * L + P * c
                nc.tensor.matmul(
                    out=bias_t[:, c : c + 1],
                    lhsT=bias_row[:, first : first + P],
                    rhs=identity_bf[:, 0:1],
                    start=True,
                    stop=True,
                )
            bias_cols[gate] = keep.tile([P, CHUNKS], F32, name="bias_cols%d" % gate)
            nc.vector.tensor_copy(out=bias_cols[gate][:], in_=bias_t[:])

        ghb_z = keep.tile([P, L], F32)
        for first, width in Z_PIECES:
            nc.vector.tensor_add(
                out=ghb_z[:, first : first + width],
                in0=bias_z[first][:],
                in1=gh_rz[:, L + first : L + first + width],
            )
        turn_bias(GATE_R, "k7")
        multiply(GATE_R, ("k0", "k1", "k2"))
        multiply_z()
        turn_gh(GATE_N, gh_n, "k7")
        multiply(GATE_N, ("k0", "k1", "k2"))

        pre_r = keep.tile([P, CHUNKS, P], F32)
        pre_n = keep.tile([P, CHUNKS, P], F32)
        pre_z = keep.tile([P, L], F32)
        gate_r = keep.tile([P, CHUNKS, P], F32)
        gate_n = keep.tile([P, CHUNKS, P], F32)
        gate_z = keep.tile([P, L], F32)
        r_gh = keep.tile([P, CHUNKS, P], F32)
        part_n = keep.tile([P, L], F32)
        z_h = keep.tile([P, L], F32)
        blend = keep.tile([P, L], F32)

        A, B, C = range(len(PIECES))

        def chunks_of(piece):
            first, count = PIECES[piece]
            return slice(first, first + count)

        def cols_of(piece):
            first, count = PIECES[piece]
            return slice(P * first, P * (first + count))

        def add_gi(out_tile, gate, piece, other):
            nc.vector.tensor_add(
                out=out_tile[:, chunks_of(piece), :],
                in0=gi[(gate, PIECES[piece][0])][:],
                in1=other[:, chunks_of(piece), :],
            )

        def act(out_tile, in_tile, gate, func, piece):
            first, count = PIECES[piece]
            for c in range(first, first + count):
                nc.scalar.activation(
                    out=out_tile[:, c, :],
                    in_=in_tile[:, c, :],
                    func=func,
                    bias=bias_cols[gate][:, c : c + 1],
                )

        def gate_z_of(piece):
            first, width = Z_PIECES[piece]
            cols = slice(first, first + width)
            nc.vector.tensor_add(out=pre_z[:, cols], in0=gi[(GATE_Z, first)][:], in1=ghb_z[:, cols])
            nc.scalar.activation(out=gate_z[:, cols], in_=pre_z[:, cols], func=ACT.Sigmoid)

        def times_gh_n(piece):
            nc.vector.tensor_mul(
                out=r_gh[:, chunks_of(piece), :],
                in0=gate_r[:, chunks_of(piece), :],
                in1=gh_t[GATE_N][:, chunks_of(piece), :],
            )

        n_back = {}

        def turn_back(piece, tag):
            first, count = PIECES[piece]
            n_back[piece] = psum.tile([P, count, P], F32, name="n_back%d" % piece, tag=tag)
            for c in range(first, first + count):
                nc.tensor.transpose(n_back[piece][:, c - first, :], gate_n[:, c, :], identity[:])

        def times_h(engine, piece):
            cols = cols_of(piece)
            engine.tensor_mul(out=z_h[:, cols], in0=gate_z[:, cols], in1=h_sb[:, cols])

        def minus_part_n(piece):
            cols = cols_of(piece)
            nc.vector.scalar_tensor_tensor(
                out=part_n[:, cols],
                in0=gate_z[:, cols],
                scalar=1.0,
                in1=n_back[piece][:].rearrange("p c b -> p (c b)"),
                op0=ALU.subtract,
                op1=ALU.mult,
            )

        def finish(piece):
            cols = cols_of(piece)
            nc.vector.tensor_sub(out=blend[:, cols], in0=z_h[:, cols], in1=part_n[:, cols])
            nc.sync.dma_start(out=out[:, cols], in_=blend[:, cols])

        for piece in (A, B, C):
            add_gi(pre_r, GATE_R, piece, gh_r_t)
            act(gate_r, pre_r, GATE_R, ACT.Sigmoid, piece)
        gate_z_of(0)
        times_gh_n(A)
        times_gh_n(B)
        gate_z_of(1)
        times_gh_n(C)
        turn_bias(GATE_N, "k6")
        times_h(nc.gpsimd, A)
        times_h(nc.gpsimd, B)
        for piece in (A, B, C):
            add_gi(pre_n, GATE_N, piece, r_gh)
            act(gate_n, pre_n, GATE_N, ACT.Tanh, piece)
        times_h(nc.vector, C)
        turn_back(A, "k3")
        turn_back(B, "k4")
        turn_back(C, "k5")
        minus_part_n(A)
        minus_part_n(B)
        finish(A)
        minus_part_n(C)
        finish(B)
        finish(C)
